import numpy as np
import ml_dtypes


def mxq(x, axis, fmt="e4m3"):
    dtype, down = {"e4m3": (ml_dtypes.float8_e4m3fn, 7), "e5m2": (ml_dtypes.float8_e5m2, 14)}[fmt]
    v = np.moveaxis(np.asarray(x, np.float32).astype(ml_dtypes.bfloat16).astype(np.float64), axis, -1)
    blocks = v.reshape(v.shape[:-1] + (-1, 32))
    amax = np.abs(blocks).max(-1, keepdims=True)
    byte = np.maximum(np.where(amax > 0, np.frexp(amax)[1] - 1 + 127, 0) - down, 1)
    scale = np.exp2(byte - 127.0)
    codes = (blocks / scale).astype(np.float32).astype(dtype).astype(np.float64)
    return np.moveaxis((codes * scale).reshape(v.shape), -1, axis)


WIDE = False


def mx_kscale(k):
    if not WIDE:
        return np.ones(k)
    levels = np.array([10, -10, 5, -5, 0])
    a = np.random.permutation(np.resize(levels, k // 512 * 4)).reshape(k // 512, 4)
    idx = np.arange(k)
    return np.exp2(a[idx // 512, idx % 128 // 32])


BF16 = ml_dtypes.bfloat16


def bf(x):
    return np.asarray(x, np.float32).astype(BF16)


def f64(x):
    return np.asarray(x).astype(np.float64)


E2M1 = np.array([0.0, 0.5, 1.0, 1.5, 2.0, 3.0, 4.0, 6.0, -0.0, -0.5, -1.0, -1.5, -2.0, -3.0, -4.0, -6.0])


def pack_weight(w, fmt):
    k, n = w.shape
    w = f64(bf(w)).reshape(k // 32, 32, n)
    amax = np.abs(w).max(1)
    if fmt == "e4m3":
        byte = np.frexp(amax)[1] - 1 + 127 - 7
    else:
        mant, ex = np.frexp(amax / 6.0)
        byte = np.where(mant > 0.5, ex, ex - 1) + 127
    byte = np.clip(np.where(amax > 0, byte, 1), 1, 254)
    scaled = (w * np.exp2(127.0 - byte)[:, None, :]).reshape(k, n).astype(np.float32)
    by_word = np.ascontiguousarray(scaled.reshape(k // 512, 128, 4, n).transpose(0, 1, 3, 2))
    if fmt == "e4m3":
        words = by_word.astype(ml_dtypes.float8_e4m3fn).view(np.uint8)
    else:
        c = by_word.astype(ml_dtypes.float4_e2m1fn).view(np.uint8) & 0xF
        words = c[..., 0::2] | (c[..., 1::2] << 4)
    return np.ascontiguousarray(words), np.ascontiguousarray(byte.astype(np.uint8).reshape(k // 512, 16, n))


def unpack_weight(words, scales, fmt):
    g, p, n, _ = words.shape
    if fmt == "e4m3":
        vals = np.ascontiguousarray(words).view(ml_dtypes.float8_e4m3fn).astype(np.float64)
    else:
        nib = np.empty((g, p, n, 4), np.uint8)
        nib[..., 0::2] = words & 0xF
        nib[..., 1::2] = words >> 4
        vals = E2M1[nib]
    vals = vals * np.repeat(np.exp2(scales.astype(np.float64) - 127.0), 8, axis=1)[..., None]
    return vals.transpose(0, 1, 3, 2).reshape(g * 512, n)


B, S, K, IN, HID, OUT = 4, 32, 16, 1024, 512, 511
LN_EPS = 1e-5
LINK_EPS = 1e-8
FMT = "e4m3"


def sigmoid(v):
    return 1.0 / (1.0 + np.exp(-v))


def setup_inputs():
    s, t = mx_kscale(IN), mx_kscale(HID)
    keep = np.random.random((B, S, 1, 1)) > 0.125
    net_in = bf(np.random.standard_normal((B, S, K, IN)) * s)
    embeds = bf(np.random.standard_normal((B, S, OUT)) * 0.5)
    m = bf(np.random.random((B, S, K, 1)) * keep)
    W1_words, W1_scales = pack_weight(np.random.standard_normal((IN, HID)) / np.sqrt(IN) / s[:, None] * t, FMT)
    b1 = bf(np.random.standard_normal(HID) * 0.3 * t)
    Wf_words, Wf_scales = pack_weight(np.random.standard_normal((HID, OUT + 1)) * 3.0 / np.sqrt(HID) / t[:, None], FMT)
    b_f = bf(np.random.standard_normal(OUT + 1) * 0.3)
    gamma = bf(1.0 + 0.1 * np.random.standard_normal(OUT))
    beta = bf(0.1 * np.random.standard_normal(OUT))
    return {"net_in": net_in,
            "embeds": embeds,
            "m": m,
            "W1_words": W1_words,
            "W1_scales": W1_scales,
            "b1": b1,
            "Wf_words": Wf_words,
            "Wf_scales": Wf_scales,
            "b_f": b_f,
            "gamma": gamma,
            "beta": beta}


def reference(net_in, embeds, m, W1_words, W1_scales, b1, Wf_words, Wf_scales, b_f, gamma, beta):
    h = np.maximum((mxq(f64(net_in), 3, "e4m3") @ unpack_weight(W1_words, W1_scales, FMT)) + f64(b1), 0.0)
    out = (mxq(h, 3, "e4m3") @ unpack_weight(Wf_words, Wf_scales, FMT)) + f64(b_f)
    out = np.concatenate([out[..., :-1], sigmoid(out[..., -1:])], axis=-1)
    out = f64(m) * out
    link_weight = out[..., -1] + LINK_EPS
    norm = link_weight.sum(axis=2, keepdims=True)
    weights = (link_weight / norm)[..., None]
    updates = (out * weights).sum(axis=2)
    upd_weights = updates[..., -1:]
    embeds_new = f64(embeds) + upd_weights * updates[..., :-1]
    mu = embeds_new.mean(axis=-1, keepdims=True)
    var = ((embeds_new - mu) ** 2).mean(axis=-1, keepdims=True)
    return (embeds_new - mu) / np.sqrt(var + LN_EPS) * f64(gamma) + f64(beta)

@@ -1,0 +1,331 @@
+from contextlib import ExitStack
+
+import concourse.mybir as mybir
+from concourse.masks import make_identity
+
+F32 = mybir.dt.float32
+BF16 = mybir.dt.bfloat16
+I32 = mybir.dt.int32
+U32 = mybir.dt.uint32
+U8 = mybir.dt.uint8
+FP8X4 = mybir.dt.float8_e4m3fn_x4
+ALU = mybir.AluOpType
+ACT = mybir.ActivationFunctionType
+AXIS = mybir.AxisListType
+
+P = 128
+LINKS = 16
+IN = 1024
+HID = 512
+CHANNELS = 512
+FEATURES = CHANNELS - 1
+K_PASS = 512
+IN_PASSES = IN // K_PASS
+LN_EPS = 1e-5
+LINK_EPS = 1e-8
+
+LINKS_PER_LOAD = 1
+LINKS_PER_ROUND = 1
+ROUNDS = LINKS // LINKS_PER_ROUND
+BIAS_STEP = 1
+
+FLOPS = 2 * P * LINKS * (IN * HID + HID * CHANNELS)
+
+
+def tile_embed_update_pa_kernel(
+    tc, net_in, embeds, m, W1_words, W1_scales, b1, Wf_words, Wf_scales, b_f, gamma, beta, out
+):
+    nc = tc.nc
+    with ExitStack() as stack:
+        consts = stack.enter_context(tc.tile_pool(name="consts", bufs=1))
+        work = stack.enter_context(tc.tile_pool(name="work", bufs=2))
+        psum = stack.enter_context(tc.psum_pool(name="psum", bufs=2))
+        stack.enter_context(tc.manual_schedule())
+
+        x_dram = net_in.rearrange("b s l k -> (b s) l k")
+        x_sb = []
+        for i in range(LINKS // LINKS_PER_LOAD):
+            x_sb.append(consts.tile([P, LINKS_PER_LOAD, IN], BF16, name="x%d" % i))
+
+        def load_x(i):
+            links = slice(i * LINKS_PER_LOAD, (i + 1) * LINKS_PER_LOAD)
+            nc.sync.dma_start(out=x_sb[i][:], in_=x_dram[:, links, :])
+
+        planes = consts.tile([P, IN_PASSES + 1, HID], U8, align_bytes=64)
+        nc.vector.memset(planes[:].bitcast(I32), 0)
+        rows = consts.tile([P, 2, HID], BF16)
+        nc.vector.memset(rows[:], 0.0)
+        ones = consts.tile([P, P], BF16)
+        nc.gpsimd.memset(ones[:], 1.0)
+        ident = consts.tile([P, P], F32)
+        make_identity(nc, ident[:])
+        minus_half = consts.tile([P, 1], F32)
+        nc.gpsimd.memset(minus_half[:], -0.5)
+
+        w1_words = consts.tile([P, IN_PASSES, HID], U32, align_bytes=64)
+        wf_words = consts.tile([P, CHANNELS], U32, align_bytes=64)
+        m_sb = consts.tile([P, LINKS], BF16)
+        emb_sb = consts.tile([P, FEATURES], BF16)
+        gamma_bc = consts.tile([P, FEATURES], BF16)
+        beta_bc = consts.tile([P, FEATURES], BF16)
+
+        load_x(0)
+        nc.scalar.dma_start(out=rows[0:1, 0, :], in_=b1.rearrange("(o n) -> o n", o=1))
+        nc.scalar.dma_start(out=rows[0:1, 1, :], in_=b_f.rearrange("(o n) -> o n", o=1))
+        nc.scalar.dma_start(out=m_sb[:], in_=m.rearrange("b s l o -> (b s) (l o)"))
+        w1_rows = W1_scales.rearrange("g (q r) n -> r q g n", r=4)
+        for r in range(4):
+            nc.sync.dma_start(
+                out=planes[r:P:32, 0:IN_PASSES, :].bitcast(I32), in_=w1_rows[r].bitcast(I32)
+            )
+        load_x(1)
+        load_x(2)
+        nc.sync.dma_start(
+            out=w1_words[:].bitcast(I32),
+            in_=W1_words.rearrange("g p n t -> p g (n t)").bitcast(I32),
+        )
+        load_x(3)
+        load_x(4)
+        wf_rows = Wf_scales.rearrange("g (q r) n -> r q (g n)", r=4)
+        for r in range(4):
+            nc.sync.dma_start(
+                out=planes[r:P:32, IN_PASSES, :].bitcast(I32), in_=wf_rows[r].bitcast(I32)
+            )
+        nc.sync.dma_start(
+            out=wf_words[:].bitcast(I32),
+            in_=Wf_words.rearrange("g p n t -> p (g n t)").bitcast(I32),
+        )
+        for i in range(5, LINKS // LINKS_PER_LOAD):
+            load_x(i)
+        nc.sync.dma_start(out=emb_sb[:], in_=embeds.rearrange("b s c -> (b s) c"))
+        nc.sync.dma_start(out=gamma_bc[:], in_=gamma.partition_broadcast(P))
+        nc.sync.dma_start(out=beta_bc[:], in_=beta.partition_broadcast(P))
+
+        table_warm = consts.tile([P, 1], F32)
+        nc.scalar.activation(out=table_warm[:], in_=minus_half[:], func=ACT.Sigmoid)
+
+        m_sq = consts.tile([P, LINKS], F32)
+        nc.gpsimd.tensor_tensor(out=m_sq[:], in0=m_sb[:], in1=m_sb[:], op=ALU.mult)
+        m_eps = consts.tile([P, LINKS], F32)
+        nc.gpsimd.tensor_scalar(
+            out=m_eps[:], in0=m_sb[:], scalar1=LINK_EPS, scalar2=0.0, op0=ALU.mult, op1=ALU.add
+        )
+
+        b1_bc = consts.tile([P, 2, P, 2], F32)
+        bf_bc = consts.tile([P, CHANNELS], F32)
+
+        def spread_biases():
+            b1_ps = psum.tile([P, HID], F32, tag="o_ps")
+            nc.tensor.matmul(out=b1_ps[:], lhsT=ones[:], rhs=rows[:, 0, :], start=True, stop=True)
+            nc.vector.tensor_copy(
+                out=b1_bc[:], in_=b1_ps[:].rearrange("r (p u e) -> r u p e", u=2, e=2)
+            )
+            bf_ps = psum.tile([P, CHANNELS], F32, tag="o_ps")
+            nc.tensor.matmul(out=bf_ps[:], lhsT=ones[:], rhs=rows[:, 1, :], start=True, stop=True)
+            nc.vector.tensor_copy(out=bf_bc[:], in_=bf_ps[:])
+
+        sig = consts.tile([P, LINKS], F32)
+        terms = consts.tile([P, 3, LINKS], F32)
+        acc = consts.tile([P, FEATURES], F32)
+        xt_ps, x_grouped, x_codes, x_scales = {}, {}, {}, {}
+        h_ps, h_sorted, ht_ps, h_grouped, h_codes, h_scales, o_ps = {}, {}, {}, {}, {}, {}, {}
+        bufs = 3 * LINKS_PER_ROUND
+
+        def links_of(rnd):
+            if 0 <= rnd < ROUNDS:
+                return range(rnd * LINKS_PER_ROUND, (rnd + 1) * LINKS_PER_ROUND)
+            return range(0)
+
+        def transpose_x(rnd):
+            for j in links_of(rnd):
+                words = x_sb[j // LINKS_PER_LOAD][:, j % LINKS_PER_LOAD, :].bitcast(F32)
+                xt_ps[j] = psum.tile([P, IN_PASSES, 2, P], F32, name="xt_ps")
+                for g in range(IN_PASSES):
+                    for u in range(2):
+                        first = g * (K_PASS // 2) + u
+                        nc.tensor.transpose(
+                            xt_ps[j][:, g, u, :], words[:, first : (g + 1) * (K_PASS // 2) : 2], ident[:]
+                        )
+
+        def regroup_x(rnd):
+            for j in links_of(rnd):
+                x_grouped[j] = work.tile(
+                    [P, IN_PASSES, P, 4], BF16, name="x_grouped", bufs=bufs, align_bytes=64
+                )
+                nc.scalar.copy(
+                    out=x_grouped[j][:].bitcast(F32), in_=xt_ps[j][:].rearrange("p g u r -> p g r u")
+                )
+
+        def quantise_x(rnd):
+            for j in links_of(rnd):
+                x_codes[j] = work.tile([P, IN_PASSES, P], U32, name="x_codes", bufs=bufs, align_bytes=64)
+                x_scales[j] = work.tile([P, IN_PASSES, P], U8, name="x_scales", bufs=bufs, align_bytes=64)
+                nc.vector.quantize_mx(
+                    out=x_codes[j][:].rearrange("p g r -> p (g r)").bitcast(FP8X4),
+                    scales=x_scales[j][:].rearrange("p g r -> p (g r)"),
+                    in_=x_grouped[j][:].rearrange("p g r t -> p (g r t)"),
+                )
+
+        def first_matmul(rnd):
+            for j in links_of(rnd):
+                h_ps[j] = psum.tile([P, HID], F32, name="h_ps")
+                for g in range(IN_PASSES):
+                    nc.tensor.matmul_mx(
+                        out=h_ps[j][:],
+                        lhsT=x_codes[j][:, g, :].bitcast(FP8X4),
+                        lhsT_scale=x_scales[j][:, g, :],
+                        rhs=w1_words[:, g, :].bitcast(FP8X4),
+                        rhs_scale=planes[:, g, :],
+                        start=(g == 0),
+                        stop=(g == IN_PASSES - 1),
+                    )
+
+        def add_bias(rnd):
+            for j in links_of(rnd):
+                h_sorted[j] = work.tile([P, 2, P, 2], BF16, name="h_sorted", bufs=bufs)
+                nc.vector.tensor_tensor(
+                    out=h_sorted[j][:],
+                    in0=h_ps[j][:].rearrange("r (p u e) -> r u p e", u=2, e=2),
+                    in1=b1_bc[:],
+                    op=ALU.add,
+                )
+
+        def transpose_h(rnd):
+            if len(links_of(rnd)) == 0:
+                return
+            ht_ps[rnd] = psum.tile([P, 2, LINKS_PER_ROUND, P], F32, name="ht_ps")
+            for i, j in enumerate(links_of(rnd)):
+                for u in range(2):
+                    nc.tensor.transpose(
+                        ht_ps[rnd][:, u, i, :],
+                        h_sorted[j][:, u, :, :].rearrange("r p e -> r (p e)").bitcast(F32),
+                        ident[:],
+                    )
+
+        def relu_h(rnd):
+            if len(links_of(rnd)) == 0:
+                return
+            h_grouped[rnd] = work.tile([P, LINKS_PER_ROUND * P, 4], BF16, name="h_grouped", bufs=3, align_bytes=64)
+            nc.scalar.activation(
+                out=h_grouped[rnd][:].rearrange("p c (u e) -> p c u e", e=2),
+                in_=ht_ps[rnd][:]
+                .rearrange("p u i r -> p u (i r)")
+                .bitcast(BF16)
+                .rearrange("p u (c e) -> p c u e", e=2),
+                func=ACT.Relu,
+            )
+
+        def quantise_h(rnd):
+            if len(links_of(rnd)) == 0:
+                return
+            h_codes[rnd] = work.tile([P, LINKS_PER_ROUND * P], U32, name="h_codes", bufs=3, align_bytes=64)
+            h_scales[rnd] = work.tile([P, LINKS_PER_ROUND * P], U8, name="h_scales", bufs=3, align_bytes=64)
+            nc.vector.quantize_mx(
+                out=h_codes[rnd][:].bitcast(FP8X4),
+                scales=h_scales[rnd][:],
+                in_=h_grouped[rnd][:].rearrange("p c t -> p (c t)"),
+            )
+
+        def second_matmul(rnd):
+            for i, j in enumerate(links_of(rnd)):
+                tokens = slice(i * P, (i + 1) * P)
+                o_ps[j] = psum.tile([P, CHANNELS], F32, name="o_ps")
+                nc.tensor.matmul_mx(
+                    out=o_ps[j][:],
+                    lhsT=h_codes[rnd][:, tokens].bitcast(FP8X4),
+                    lhsT_scale=h_scales[rnd][:, tokens],
+                    rhs=wf_words[:].bitcast(FP8X4),
+                    rhs_scale=planes[:, IN_PASSES, :],
+                    start=True,
+                    stop=True,
+                )
+
+        def gate(rnd):
+            for j in links_of(rnd):
+                nc.scalar.activation(
+                    out=sig[:, j : j + 1],
+                    in_=o_ps[j][:, FEATURES:CHANNELS],
+                    func=ACT.Sigmoid,
+                    bias=bf_bc[:, FEATURES:CHANNELS],
+                )
+                nc.scalar.activation(
+                    out=terms[:, 2, j : j + 1],
+                    in_=sig[:, j : j + 1],
+                    func=ACT.Identity,
+                    scale=m_sq[:, j : j + 1],
+                    bias=m_eps[:, j : j + 1],
+                )
+
+        def pool_links(rnd):
+            for j in links_of(rnd):
+                if j == 0:
+                    nc.vector.tensor_scalar_mul(
+                        out=acc[:], in0=o_ps[j][:, 0:FEATURES], scalar1=terms[:, 2, j : j + 1]
+                    )
+                else:
+                    nc.vector.scalar_tensor_tensor(
+                        out=acc[:],
+                        in0=o_ps[j][:, 0:FEATURES],
+                        scalar=terms[:, 2, j : j + 1],
+                        in1=acc[:],
+                        op0=ALU.mult,
+                        op1=ALU.add,
+                    )
+
+        for step in range(ROUNDS + 8):
+            transpose_x(step)
+            regroup_x(step)
+            transpose_h(step - 4)
+            relu_h(step - 4)
+            first_matmul(step - 2)
+            second_matmul(step - 6)
+            gate(step - 6)
+            quantise_x(step - 1)
+            add_bias(step - 3)
+            quantise_h(step - 5)
+            pool_links(step - 7)
+            if step == BIAS_STEP:
+                spread_biases()
+
+        g_all = consts.tile([P, LINKS], F32)
+        nc.gpsimd.tensor_tensor(out=g_all[:], in0=sig[:], in1=m_sb[:], op=ALU.mult)
+        nc.gpsimd.tensor_scalar(
+            out=terms[:, 0, :], in0=g_all[:], scalar1=1.0, scalar2=LINK_EPS, op0=ALU.mult, op1=ALU.add
+        )
+        nc.gpsimd.tensor_tensor(out=terms[:, 1, :], in0=terms[:, 0, :], in1=g_all[:], op=ALU.mult)
+        sums = consts.tile([P, 3], F32)
+        nc.vector.tensor_reduce(out=sums[:], in_=terms[:], axis=AXIS.X, op=ALU.add)
+        inv_l = consts.tile([P, 1], F32)
+        nc.vector.reciprocal(out=inv_l[:], in_=sums[:, 0:1])
+        scale = consts.tile([P, 1], F32)
+        nc.vector.tensor_scalar(
+            out=scale[:], in0=sums[:, 1:2], scalar1=inv_l[:], scalar2=inv_l[:], op0=ALU.mult, op1=ALU.mult
+        )
+        bias_scale = consts.tile([P, 1], F32)
+        nc.vector.tensor_tensor(out=bias_scale[:], in0=sums[:, 2:3], in1=scale[:], op=ALU.mult)
+        base = consts.tile([P, FEATURES], F32)
+        nc.vector.scalar_tensor_tensor(
+            out=base[:], in0=bf_bc[:, 0:FEATURES], scalar=bias_scale[:], in1=emb_sb[:], op0=ALU.mult, op1=ALU.add
+        )
+        e_new = consts.tile([P, FEATURES], F32)
+        nc.vector.scalar_tensor_tensor(
+            out=e_new[:], in0=acc[:], scalar=scale[:], in1=base[:], op0=ALU.mult, op1=ALU.add
+        )
+
+        stats = consts.tile([P, 6], F32)
+        nc.vector.bn_stats(out=stats[:], in_=e_new[:])
+        mean_var = consts.tile([P, 2], F32)
+        nc.vector.bn_aggr(out=mean_var[:], in_=stats[:])
+        var_eps = consts.tile([P, 1], F32)
+        nc.vector.tensor_scalar_add(out=var_eps[:], in0=mean_var[:, 1:2], scalar1=LN_EPS)
+        rstd = consts.tile([P, 1], F32)
+        nc.gpsimd.tensor_tensor(out=rstd[:], in0=var_eps[:], in1=minus_half[:], op=ALU.pow)
+        centred = consts.tile([P, FEATURES], F32)
+        nc.vector.scalar_tensor_tensor(
+            out=centred[:], in0=e_new[:], scalar=mean_var[:, 0:1], in1=gamma_bc[:], op0=ALU.subtract, op1=ALU.mult
+        )
+        result = consts.tile([P, FEATURES], F32)
+        nc.vector.scalar_tensor_tensor(
+            out=result[:], in0=centred[:], scalar=rstd[:], in1=beta_bc[:], op0=ALU.mult, op1=ALU.add
+        )
+        nc.sync.dma_start(out=out.rearrange("b s c -> (b s) c"), in_=result[:])

@@ -19,15 +19,17 @@ IN = 1024
 HID = 512
 CHANNELS = 512
 FEATURES = CHANNELS - 1
-K_PASS = 512
+PACK = 4
+K_PASS = P * PACK
 IN_PASSES = IN // K_PASS
 LN_EPS = 1e-5
 LINK_EPS = 1e-8
 
-LINKS_PER_LOAD = 1
-LINKS_PER_ROUND = 1
-ROUNDS = LINKS // LINKS_PER_ROUND
-BIAS_STEP = 1
+BLOCK_LINKS = 2
+BLOCKS = LINKS // BLOCK_LINKS
+ROWS = BLOCK_LINKS * P
+M1_LAG = 1
+M2_LAG = 2
 
 FLOPS = 2 * P * LINKS * (IN * HID + HID * CHANNELS)
 
@@ -38,54 +40,47 @@ def tile_embed_update_pa_kernel(
     nc = tc.nc
     with ExitStack() as stack:
         consts = stack.enter_context(tc.tile_pool(name="consts", bufs=1))
-        work = stack.enter_context(tc.tile_pool(name="work", bufs=2))
+        work = stack.enter_context(tc.tile_pool(name="work", bufs=3))
         psum = stack.enter_context(tc.psum_pool(name="psum", bufs=2))
         stack.enter_context(tc.manual_schedule())
 
         x_dram = net_in.rearrange("b s l k -> (b s) l k")
         x_sb = []
-        for i in range(LINKS // LINKS_PER_LOAD):
-            x_sb.append(consts.tile([P, LINKS_PER_LOAD, IN], BF16, name="x%d" % i))
+        for j in range(LINKS):
+            x_sb.append(consts.tile([P, IN], BF16, name="x%d" % j))
 
-        def load_x(i):
-            links = slice(i * LINKS_PER_LOAD, (i + 1) * LINKS_PER_LOAD)
-            nc.sync.dma_start(out=x_sb[i][:], in_=x_dram[:, links, :])
+        def load_x(j):
+            nc.sync.dma_start(out=x_sb[j][:], in_=x_dram[:, j, :])
 
         planes = consts.tile([P, IN_PASSES + 1, HID], U8, align_bytes=64)
         nc.vector.memset(planes[:].bitcast(I32), 0)
-        rows = consts.tile([P, 2, HID], BF16)
-        nc.vector.memset(rows[:], 0.0)
-        ones = consts.tile([P, P], BF16)
-        nc.gpsimd.memset(ones[:], 1.0)
         ident = consts.tile([P, P], F32)
         make_identity(nc, ident[:])
         minus_half = consts.tile([P, 1], F32)
         nc.gpsimd.memset(minus_half[:], -0.5)
 
-        w1_words = consts.tile([P, IN_PASSES, HID], U32, align_bytes=64)
+        w1_raw = consts.tile([P, IN_PASSES, HID], I32)
         wf_words = consts.tile([P, CHANNELS], U32, align_bytes=64)
         m_sb = consts.tile([P, LINKS], BF16)
+        b1_sb = consts.tile([P, PACK], BF16)
+        bf_bc = consts.tile([P, CHANNELS], BF16)
         emb_sb = consts.tile([P, FEATURES], BF16)
         gamma_bc = consts.tile([P, FEATURES], BF16)
         beta_bc = consts.tile([P, FEATURES], BF16)
 
-        load_x(0)
-        nc.scalar.dma_start(out=rows[0:1, 0, :], in_=b1.rearrange("(o n) -> o n", o=1))
-        nc.scalar.dma_start(out=rows[0:1, 1, :], in_=b_f.rearrange("(o n) -> o n", o=1))
+        nc.scalar.dma_start(out=b1_sb[:], in_=b1.rearrange("(p t) -> p t", t=PACK))
         nc.scalar.dma_start(out=m_sb[:], in_=m.rearrange("b s l o -> (b s) (l o)"))
         w1_rows = W1_scales.rearrange("g (q r) n -> r q g n", r=4)
         for r in range(4):
             nc.sync.dma_start(
                 out=planes[r:P:32, 0:IN_PASSES, :].bitcast(I32), in_=w1_rows[r].bitcast(I32)
             )
-        load_x(1)
-        load_x(2)
-        nc.sync.dma_start(
-            out=w1_words[:].bitcast(I32),
-            in_=W1_words.rearrange("g p n t -> p g (n t)").bitcast(I32),
-        )
-        load_x(3)
-        load_x(4)
+        for g in range(IN_PASSES):
+            nc.sync.dma_start(
+                out=w1_raw[:, g, :], in_=W1_words[g].rearrange("p n t -> p (n t)").bitcast(I32)
+            )
+        for j in range(6):
+            load_x(j)
         wf_rows = Wf_scales.rearrange("g (q r) n -> r q (g n)", r=4)
         for r in range(4):
             nc.sync.dma_start(
@@ -95,8 +90,11 @@ def tile_embed_update_pa_kernel(
             out=wf_words[:].bitcast(I32),
             in_=Wf_words.rearrange("g p n t -> p (g n t)").bitcast(I32),
         )
-        for i in range(5, LINKS // LINKS_PER_LOAD):
-            load_x(i)
+        load_x(6)
+        load_x(7)
+        nc.sync.dma_start(out=bf_bc[:], in_=b_f.partition_broadcast(P))
+        for j in range(8, LINKS):
+            load_x(j)
         nc.sync.dma_start(out=emb_sb[:], in_=embeds.rearrange("b s c -> (b s) c"))
         nc.sync.dma_start(out=gamma_bc[:], in_=gamma.partition_broadcast(P))
         nc.sync.dma_start(out=beta_bc[:], in_=beta.partition_broadcast(P))
@@ -111,34 +109,33 @@ def tile_embed_update_pa_kernel(
             out=m_eps[:], in0=m_sb[:], scalar1=LINK_EPS, scalar2=0.0, op0=ALU.mult, op1=ALU.add
         )
 
-        b1_bc = consts.tile([P, 2, P, 2], F32)
-        bf_bc = consts.tile([P, CHANNELS], F32)
-
-        def spread_biases():
-            b1_ps = psum.tile([P, HID], F32, tag="o_ps")
-            nc.tensor.matmul(out=b1_ps[:], lhsT=ones[:], rhs=rows[:, 0, :], start=True, stop=True)
+        w1_cols = consts.tile([P, IN_PASSES, PACK, P], I32, align_bytes=64)
+        w1_planes = consts.tile([P, IN_PASSES, PACK, P], U8, align_bytes=64)
+        raw_planes = planes[:, 0:IN_PASSES, :].rearrange("p g (m t) -> p g m t", t=PACK)
+        for t in range(PACK):
+            nc.vector.tensor_copy(out=w1_planes[:, :, t, :], in_=raw_planes[:, :, :, t])
+        for g in range(IN_PASSES):
             nc.vector.tensor_copy(
-                out=b1_bc[:], in_=b1_ps[:].rearrange("r (p u e) -> r u p e", u=2, e=2)
+                out=w1_cols[:, g, :, :], in_=w1_raw[:, g, :].rearrange("p (m t) -> p t m", t=PACK)
             )
-            bf_ps = psum.tile([P, CHANNELS], F32, tag="o_ps")
-            nc.tensor.matmul(out=bf_ps[:], lhsT=ones[:], rhs=rows[:, 1, :], start=True, stop=True)
-            nc.vector.tensor_copy(out=bf_bc[:], in_=bf_ps[:])
 
         sig = consts.tile([P, LINKS], F32)
         terms = consts.tile([P, 3, LINKS], F32)
         acc = consts.tile([P, FEATURES], F32)
         xt_ps, x_grouped, x_codes, x_scales = {}, {}, {}, {}
-        h_ps, h_sorted, ht_ps, h_grouped, h_codes, h_scales, o_ps = {}, {}, {}, {}, {}, {}, {}
-        bufs = 3 * LINKS_PER_ROUND
+        h_ps, h_slots, h_grouped, h_codes, h_scales, o_ps = {}, {}, {}, {}, {}, {}
 
-        def links_of(rnd):
-            if 0 <= rnd < ROUNDS:
-                return range(rnd * LINKS_PER_ROUND, (rnd + 1) * LINKS_PER_ROUND)
+        def links_of(blk):
+            if 0 <= blk < BLOCKS:
+                return range(blk * BLOCK_LINKS, (blk + 1) * BLOCK_LINKS)
             return range(0)
 
-        def transpose_x(rnd):
-            for j in links_of(rnd):
-                words = x_sb[j // LINKS_PER_LOAD][:, j % LINKS_PER_LOAD, :].bitcast(F32)
+        def transpose_x(blk):
+            if len(links_of(blk)) == 0:
+                return
+            x_grouped[blk] = work.tile([P, IN_PASSES, ROWS, PACK], BF16, name="x_grouped", align_bytes=64)
+            for i, j in enumerate(links_of(blk)):
+                words = x_sb[j][:].bitcast(F32)
                 xt_ps[j] = psum.tile([P, IN_PASSES, 2, P], F32, name="xt_ps")
                 for g in range(IN_PASSES):
                     for u in range(2):
@@ -146,102 +143,80 @@ def tile_embed_update_pa_kernel(
                         nc.tensor.transpose(
                             xt_ps[j][:, g, u, :], words[:, first : (g + 1) * (K_PASS // 2) : 2], ident[:]
                         )
-
-        def regroup_x(rnd):
-            for j in links_of(rnd):
-                x_grouped[j] = work.tile(
-                    [P, IN_PASSES, P, 4], BF16, name="x_grouped", bufs=bufs, align_bytes=64
-                )
                 nc.scalar.copy(
-                    out=x_grouped[j][:].bitcast(F32), in_=xt_ps[j][:].rearrange("p g u r -> p g r u")
+                    out=x_grouped[blk][:, :, i * P : (i + 1) * P, :].bitcast(F32),
+                    in_=xt_ps[j][:].rearrange("p g u r -> p g r u"),
                 )
 
-        def quantise_x(rnd):
-            for j in links_of(rnd):
-                x_codes[j] = work.tile([P, IN_PASSES, P], U32, name="x_codes", bufs=bufs, align_bytes=64)
-                x_scales[j] = work.tile([P, IN_PASSES, P], U8, name="x_scales", bufs=bufs, align_bytes=64)
-                nc.vector.quantize_mx(
-                    out=x_codes[j][:].rearrange("p g r -> p (g r)").bitcast(FP8X4),
-                    scales=x_scales[j][:].rearrange("p g r -> p (g r)"),
-                    in_=x_grouped[j][:].rearrange("p g r t -> p (g r t)"),
-                )
-
-        def first_matmul(rnd):
-            for j in links_of(rnd):
-                h_ps[j] = psum.tile([P, HID], F32, name="h_ps")
-                for g in range(IN_PASSES):
-                    nc.tensor.matmul_mx(
-                        out=h_ps[j][:],
-                        lhsT=x_codes[j][:, g, :].bitcast(FP8X4),
-                        lhsT_scale=x_scales[j][:, g, :],
-                        rhs=w1_words[:, g, :].bitcast(FP8X4),
-                        rhs_scale=planes[:, g, :],
-                        start=(g == 0),
-                        stop=(g == IN_PASSES - 1),
-                    )
-
-        def add_bias(rnd):
-            for j in links_of(rnd):
-                h_sorted[j] = work.tile([P, 2, P, 2], BF16, name="h_sorted", bufs=bufs)
-                nc.vector.tensor_tensor(
-                    out=h_sorted[j][:],
-                    in0=h_ps[j][:].rearrange("r (p u e) -> r u p e", u=2, e=2),
-                    in1=b1_bc[:],
-                    op=ALU.add,
-                )
-
-        def transpose_h(rnd):
-            if len(links_of(rnd)) == 0:
+        def quantise_x(blk):
+            if len(links_of(blk)) == 0:
                 return
-            ht_ps[rnd] = psum.tile([P, 2, LINKS_PER_ROUND, P], F32, name="ht_ps")
-            for i, j in enumerate(links_of(rnd)):
-                for u in range(2):
-                    nc.tensor.transpose(
-                        ht_ps[rnd][:, u, i, :],
-                        h_sorted[j][:, u, :, :].rearrange("r p e -> r (p e)").bitcast(F32),
-                        ident[:],
-                    )
-
-        def relu_h(rnd):
-            if len(links_of(rnd)) == 0:
-                return
-            h_grouped[rnd] = work.tile([P, LINKS_PER_ROUND * P, 4], BF16, name="h_grouped", bufs=3, align_bytes=64)
-            nc.scalar.activation(
-                out=h_grouped[rnd][:].rearrange("p c (u e) -> p c u e", e=2),
-                in_=ht_ps[rnd][:]
-                .rearrange("p u i r -> p u (i r)")
-                .bitcast(BF16)
-                .rearrange("p u (c e) -> p c u e", e=2),
-                func=ACT.Relu,
-            )
-
-        def quantise_h(rnd):
-            if len(links_of(rnd)) == 0:
-                return
-            h_codes[rnd] = work.tile([P, LINKS_PER_ROUND * P], U32, name="h_codes", bufs=3, align_bytes=64)
-            h_scales[rnd] = work.tile([P, LINKS_PER_ROUND * P], U8, name="h_scales", bufs=3, align_bytes=64)
+            x_codes[blk] = work.tile([P, IN_PASSES, ROWS], U32, name="x_codes", align_bytes=64)
+            x_scales[blk] = work.tile([P, IN_PASSES, ROWS], U8, name="x_scales", align_bytes=64)
             nc.vector.quantize_mx(
-                out=h_codes[rnd][:].bitcast(FP8X4),
-                scales=h_scales[rnd][:],
-                in_=h_grouped[rnd][:].rearrange("p c t -> p (c t)"),
+                out=x_codes[blk][:].rearrange("p g r -> p (g r)").bitcast(FP8X4),
+                scales=x_scales[blk][:].rearrange("p g r -> p (g r)"),
+                in_=x_grouped[blk][:].rearrange("p g r t -> p (g r t)"),
             )
 
-        def second_matmul(rnd):
-            for i, j in enumerate(links_of(rnd)):
+        def first_matmul(blk):
+            if len(links_of(blk)) == 0:
+                return
+            h_slots[blk] = work.tile([P, PACK, ROWS], BF16, name="h_slots")
+            for half in range(PACK // 2):
+                h_ps[blk, half] = psum.tile([P, 2, ROWS], F32, name="h_ps")
+                for s in range(2):
+                    t = 2 * half + s
+                    for g in range(IN_PASSES):
+                        nc.tensor.matmul_mx(
+                            out=h_ps[blk, half][:, s, :],
+                            lhsT=w1_cols[:, g, t, :].bitcast(FP8X4),
+                            lhsT_scale=w1_planes[:, g, t, :],
+                            rhs=x_codes[blk][:, g, :].bitcast(FP8X4),
+                            rhs_scale=x_scales[blk][:, g, :],
+                            start=(g == 0),
+                            stop=(g == IN_PASSES - 1),
+                        )
+                for s in range(2):
+                    t = 2 * half + s
+                    nc.scalar.activation(
+                        out=h_slots[blk][:, t, :],
+                        in_=h_ps[blk, half][:, s, :],
+                        func=ACT.Relu,
+                        bias=b1_sb[:, t : t + 1],
+                    )
+
+        def group_h(blk):
+            if len(links_of(blk)) == 0:
+                return
+            h_grouped[blk] = work.tile([P, ROWS, PACK], BF16, name="h_grouped", align_bytes=64)
+            nc.vector.tensor_copy(out=h_grouped[blk][:], in_=h_slots[blk][:].rearrange("p t r -> p r t"))
+
+        def quantise_h(blk):
+            if len(links_of(blk)) == 0:
+                return
+            h_codes[blk] = work.tile([P, ROWS], U32, name="h_codes", align_bytes=64)
+            h_scales[blk] = work.tile([P, ROWS], U8, name="h_scales", align_bytes=64)
+            nc.vector.quantize_mx(
+                out=h_codes[blk][:].bitcast(FP8X4),
+                scales=h_scales[blk][:],
+                in_=h_grouped[blk][:].rearrange("p r t -> p (r t)"),
+            )
+
+        def second_matmul(blk):
+            for i, j in enumerate(links_of(blk)):
                 tokens = slice(i * P, (i + 1) * P)
-                o_ps[j] = psum.tile([P, CHANNELS], F32, name="o_ps")
+                o_ps[j] = psum.tile([P, CHANNELS], F32, name="o_ps", bufs=4)
                 nc.tensor.matmul_mx(
                     out=o_ps[j][:],
-                    lhsT=h_codes[rnd][:, tokens].bitcast(FP8X4),
-                    lhsT_scale=h_scales[rnd][:, tokens],
+                    lhsT=h_codes[blk][:, tokens].bitcast(FP8X4),
+                    lhsT_scale=h_scales[blk][:, tokens],
                     rhs=wf_words[:].bitcast(FP8X4),
                     rhs_scale=planes[:, IN_PASSES, :],
                     start=True,
                     stop=True,
                 )
-
-        def gate(rnd):
-            for j in links_of(rnd):
+            for j in links_of(blk):
                 nc.scalar.activation(
                     out=sig[:, j : j + 1],
                     in_=o_ps[j][:, FEATURES:CHANNELS],
@@ -256,36 +231,33 @@ def tile_embed_update_pa_kernel(
                     bias=m_eps[:, j : j + 1],
                 )
 
-        def pool_links(rnd):
-            for j in links_of(rnd):
-                if j == 0:
-                    nc.vector.tensor_scalar_mul(
-                        out=acc[:], in0=o_ps[j][:, 0:FEATURES], scalar1=terms[:, 2, j : j + 1]
-                    )
-                else:
-                    nc.vector.scalar_tensor_tensor(
-                        out=acc[:],
-                        in0=o_ps[j][:, 0:FEATURES],
-                        scalar=terms[:, 2, j : j + 1],
-                        in1=acc[:],
-                        op0=ALU.mult,
-                        op1=ALU.add,
-                    )
+        def pool_link(blk, i):
+            if len(links_of(blk)) == 0:
+                return
+            j = links_of(blk)[i]
+            if j == 0:
+                nc.vector.tensor_scalar_mul(
+                    out=acc[:], in0=o_ps[j][:, 0:FEATURES], scalar1=terms[:, 2, j : j + 1]
+                )
+            else:
+                nc.vector.scalar_tensor_tensor(
+                    out=acc[:],
+                    in0=o_ps[j][:, 0:FEATURES],
+                    scalar=terms[:, 2, j : j + 1],
+                    in1=acc[:],
+                    op0=ALU.mult,
+                    op1=ALU.add,
+                )
 
-        for step in range(ROUNDS + 8):
+        for step in range(BLOCKS + M2_LAG):
             transpose_x(step)
-            regroup_x(step)
-            transpose_h(step - 4)
-            relu_h(step - 4)
-            first_matmul(step - 2)
-            second_matmul(step - 6)
-            gate(step - 6)
-            quantise_x(step - 1)
-            add_bias(step - 3)
-            quantise_h(step - 5)
-            pool_links(step - 7)
-            if step == BIAS_STEP:
-                spread_biases()
+            first_matmul(step - M1_LAG)
+            second_matmul(step - M2_LAG)
+            quantise_x(step)
+            group_h(step - M1_LAG)
+            pool_link(step - M2_LAG, 0)
+            quantise_h(step - M1_LAG)
+            pool_link(step - M2_LAG, 1)
 
         g_all = consts.tile([P, LINKS], F32)
         nc.gpsimd.tensor_tensor(out=g_all[:], in0=sig[:], in1=m_sb[:], op=ALU.mult)
@@ -301,15 +273,13 @@ def tile_embed_update_pa_kernel(
         nc.vector.tensor_scalar(
             out=scale[:], in0=sums[:, 1:2], scalar1=inv_l[:], scalar2=inv_l[:], op0=ALU.mult, op1=ALU.mult
         )
-        bias_scale = consts.tile([P, 1], F32)
-        nc.vector.tensor_tensor(out=bias_scale[:], in0=sums[:, 2:3], in1=scale[:], op=ALU.mult)
-        base = consts.tile([P, FEATURES], F32)
+        pooled = consts.tile([P, FEATURES], F32)
         nc.vector.scalar_tensor_tensor(
-            out=base[:], in0=bf_bc[:, 0:FEATURES], scalar=bias_scale[:], in1=emb_sb[:], op0=ALU.mult, op1=ALU.add
+            out=pooled[:], in0=bf_bc[:, 0:FEATURES], scalar=sums[:, 2:3], in1=acc[:], op0=ALU.mult, op1=ALU.add
         )
         e_new = consts.tile([P, FEATURES], F32)
         nc.vector.scalar_tensor_tensor(
-            out=e_new[:], in0=acc[:], scalar=scale[:], in1=base[:], op0=ALU.mult, op1=ALU.add
+            out=e_new[:], in0=pooled[:], scalar=scale[:], in1=emb_sb[:], op0=ALU.mult, op1=ALU.add
         )
 
         stats = consts.tile([P, 6], F32)

@@ -28,6 +28,7 @@ LINK_EPS = 1e-8
 BLOCK_LINKS = 2
 BLOCKS = LINKS // BLOCK_LINKS
 ROWS = BLOCK_LINKS * P
+HALF = 256
 M1_LAG = 1
 M2_LAG = 2
 
@@ -231,23 +232,22 @@ def tile_embed_update_pa_kernel(
                     bias=m_eps[:, j : j + 1],
                 )
 
-        def pool_link(blk, i):
-            if len(links_of(blk)) == 0:
-                return
-            j = links_of(blk)[i]
+        def pool_columns(j, cols):
             if j == 0:
-                nc.vector.tensor_scalar_mul(
-                    out=acc[:], in0=o_ps[j][:, 0:FEATURES], scalar1=terms[:, 2, j : j + 1]
-                )
+                nc.vector.tensor_scalar_mul(out=acc[:, cols], in0=o_ps[j][:, cols], scalar1=terms[:, 2, j : j + 1])
             else:
                 nc.vector.scalar_tensor_tensor(
-                    out=acc[:],
-                    in0=o_ps[j][:, 0:FEATURES],
+                    out=acc[:, cols],
+                    in0=o_ps[j][:, cols],
                     scalar=terms[:, 2, j : j + 1],
-                    in1=acc[:],
+                    in1=acc[:, cols],
                     op0=ALU.mult,
                     op1=ALU.add,
                 )
+
+        def pool_link(blk, i):
+            if 0 <= blk < BLOCKS - 1:
+                pool_columns(links_of(blk)[i], slice(0, FEATURES))
 
         for step in range(BLOCKS + M2_LAG):
             transpose_x(step)
@@ -259,43 +259,63 @@ def tile_embed_update_pa_kernel(
             quantise_h(step - M1_LAG)
             pool_link(step - M2_LAG, 1)
 
+        halves = (slice(0, HALF), slice(HALF, FEATURES))
         g_all = consts.tile([P, LINKS], F32)
         nc.gpsimd.tensor_tensor(out=g_all[:], in0=sig[:], in1=m_sb[:], op=ALU.mult)
         nc.gpsimd.tensor_scalar(
             out=terms[:, 0, :], in0=g_all[:], scalar1=1.0, scalar2=LINK_EPS, op0=ALU.mult, op1=ALU.add
         )
         nc.gpsimd.tensor_tensor(out=terms[:, 1, :], in0=terms[:, 0, :], in1=g_all[:], op=ALU.mult)
-        sums = consts.tile([P, 3], F32)
-        nc.vector.tensor_reduce(out=sums[:], in_=terms[:], axis=AXIS.X, op=ALU.add)
+
+        for cols in halves:
+            pool_columns(LINKS - 2, cols)
+        sum_c = consts.tile([P, 1], F32)
+        nc.vector.tensor_reduce(out=sum_c[:], in_=terms[:, 2, :], axis=AXIS.X, op=ALU.add)
+        pool_columns(LINKS - 1, halves[0])
+        sums = consts.tile([P, 2], F32)
+        nc.vector.tensor_reduce(out=sums[:], in_=terms[:, 0:2, :], axis=AXIS.X, op=ALU.add)
+        pool_columns(LINKS - 1, halves[1])
         inv_l = consts.tile([P, 1], F32)
         nc.vector.reciprocal(out=inv_l[:], in_=sums[:, 0:1])
-        scale = consts.tile([P, 1], F32)
-        nc.vector.tensor_scalar(
-            out=scale[:], in0=sums[:, 1:2], scalar1=inv_l[:], scalar2=inv_l[:], op0=ALU.mult, op1=ALU.mult
-        )
         pooled = consts.tile([P, FEATURES], F32)
-        nc.vector.scalar_tensor_tensor(
-            out=pooled[:], in0=bf_bc[:, 0:FEATURES], scalar=sums[:, 2:3], in1=acc[:], op0=ALU.mult, op1=ALU.add
-        )
+        scale = consts.tile([P, 1], F32)
+        for cols in halves:
+            nc.vector.scalar_tensor_tensor(
+                out=pooled[:, cols], in0=bf_bc[:, cols], scalar=sum_c[:], in1=acc[:, cols], op0=ALU.mult, op1=ALU.add
+            )
+            if cols == halves[0]:
+                nc.vector.tensor_scalar(
+                    out=scale[:], in0=sums[:, 1:2], scalar1=inv_l[:], scalar2=inv_l[:], op0=ALU.mult, op1=ALU.mult
+                )
         e_new = consts.tile([P, FEATURES], F32)
-        nc.vector.scalar_tensor_tensor(
-            out=e_new[:], in0=pooled[:], scalar=scale[:], in1=emb_sb[:], op0=ALU.mult, op1=ALU.add
-        )
+        for cols in halves:
+            nc.vector.scalar_tensor_tensor(
+                out=e_new[:, cols], in0=pooled[:, cols], scalar=scale[:], in1=emb_sb[:, cols], op0=ALU.mult, op1=ALU.add
+            )
 
-        stats = consts.tile([P, 6], F32)
-        nc.vector.bn_stats(out=stats[:], in_=e_new[:])
+        stats = consts.tile([P, 2, 6], F32)
+        for i, cols in enumerate(halves):
+            nc.vector.bn_stats(out=stats[:, i, :], in_=e_new[:, cols])
         mean_var = consts.tile([P, 2], F32)
-        nc.vector.bn_aggr(out=mean_var[:], in_=stats[:])
+        nc.vector.bn_aggr(out=mean_var[:], in_=stats[:].rearrange("p a b -> p (a b)"))
         var_eps = consts.tile([P, 1], F32)
         nc.vector.tensor_scalar_add(out=var_eps[:], in0=mean_var[:, 1:2], scalar1=LN_EPS)
         rstd = consts.tile([P, 1], F32)
         nc.gpsimd.tensor_tensor(out=rstd[:], in0=var_eps[:], in1=minus_half[:], op=ALU.pow)
         centred = consts.tile([P, FEATURES], F32)
-        nc.vector.scalar_tensor_tensor(
-            out=centred[:], in0=e_new[:], scalar=mean_var[:, 0:1], in1=gamma_bc[:], op0=ALU.subtract, op1=ALU.mult
-        )
+        for cols in halves:
+            nc.vector.scalar_tensor_tensor(
+                out=centred[:, cols],
+                in0=e_new[:, cols],
+                scalar=mean_var[:, 0:1],
+                in1=gamma_bc[:, cols],
+                op0=ALU.subtract,
+                op1=ALU.mult,
+            )
         result = consts.tile([P, FEATURES], F32)
-        nc.vector.scalar_tensor_tensor(
-            out=result[:], in0=centred[:], scalar=rstd[:], in1=beta_bc[:], op0=ALU.mult, op1=ALU.add
-        )
-        nc.sync.dma_start(out=out.rearrange("b s c -> (b s) c"), in_=result[:])
+        out_rows = out.rearrange("b s c -> (b s) c")
+        for cols, queue in zip(halves, (nc.sync, nc.scalar)):
+            nc.vector.scalar_tensor_tensor(
+                out=result[:, cols], in0=centred[:, cols], scalar=rstd[:], in1=beta_bc[:, cols], op0=ALU.mult, op1=ALU.add
+            )
+            queue.dma_start(out=out_rows[:, cols], in_=result[:, cols])

@@ -29,6 +29,7 @@ BLOCK_LINKS = 2
 BLOCKS = LINKS // BLOCK_LINKS
 ROWS = BLOCK_LINKS * P
 HALF = 256
+RUN = 4
 M1_LAG = 1
 M2_LAG = 2
 
@@ -191,7 +192,10 @@ def tile_embed_update_pa_kernel(
             if len(links_of(blk)) == 0:
                 return
             h_grouped[blk] = work.tile([P, ROWS, PACK], BF16, name="h_grouped", align_bytes=64)
-            nc.vector.tensor_copy(out=h_grouped[blk][:], in_=h_slots[blk][:].rearrange("p t r -> p r t"))
+            nc.vector.tensor_copy(
+                out=h_grouped[blk][:].rearrange("p (c i) t -> p c t i", i=RUN),
+                in_=h_slots[blk][:].rearrange("p t (c i) -> p c t i", i=RUN),
+            )
 
         def quantise_h(blk):
             if len(links_of(blk)) == 0:

@@ -60,6 +60,10 @@ def tile_embed_update_pa_kernel(
         make_identity(nc, ident[:])
         minus_half = consts.tile([P, 1], F32)
         nc.gpsimd.memset(minus_half[:], -0.5)
+        ln_eps = consts.tile([P, 1], F32)
+        nc.gpsimd.tensor_scalar(
+            out=ln_eps[:], in0=minus_half[:], scalar1=0.0, scalar2=LN_EPS, op0=ALU.mult, op1=ALU.add
+        )
 
         w1_raw = consts.tile([P, IN_PASSES, HID], I32)
         wf_words = consts.tile([P, CHANNELS], U32, align_bytes=64)
@@ -264,28 +268,24 @@ def tile_embed_update_pa_kernel(
             pool_link(step - M2_LAG, 1)
 
         halves = (slice(0, HALF), slice(HALF, FEATURES))
+        nc.scalar.activation(out=table_warm[:], in_=ln_eps[:], func=ACT.Abs_reciprocal_sqrt)
         g_all = consts.tile([P, LINKS], F32)
-        nc.gpsimd.tensor_tensor(out=g_all[:], in0=sig[:], in1=m_sb[:], op=ALU.mult)
-        nc.gpsimd.tensor_scalar(
-            out=terms[:, 0, :], in0=g_all[:], scalar1=1.0, scalar2=LINK_EPS, op0=ALU.mult, op1=ALU.add
-        )
-        nc.gpsimd.tensor_tensor(out=terms[:, 1, :], in0=terms[:, 0, :], in1=g_all[:], op=ALU.mult)
-
-        for cols in halves:
-            pool_columns(LINKS - 2, cols)
-        sum_c = consts.tile([P, 1], F32)
-        nc.vector.tensor_reduce(out=sum_c[:], in_=terms[:, 2, :], axis=AXIS.X, op=ALU.add)
+        sums = consts.tile([P, 3], F32)
+        pool_columns(LINKS - 2, halves[0])
+        nc.vector.tensor_tensor(out=g_all[:], in0=sig[:], in1=m_sb[:], op=ALU.mult)
+        pool_columns(LINKS - 2, halves[1])
+        nc.vector.tensor_scalar_add(out=terms[:, 0, :], in0=g_all[:], scalar1=LINK_EPS)
         pool_columns(LINKS - 1, halves[0])
-        sums = consts.tile([P, 2], F32)
-        nc.vector.tensor_reduce(out=sums[:], in_=terms[:, 0:2, :], axis=AXIS.X, op=ALU.add)
+        nc.vector.tensor_tensor(out=terms[:, 1, :], in0=terms[:, 0, :], in1=g_all[:], op=ALU.mult)
         pool_columns(LINKS - 1, halves[1])
+        nc.vector.tensor_reduce(out=sums[:], in_=terms[:], axis=AXIS.X, op=ALU.add)
         inv_l = consts.tile([P, 1], F32)
         nc.vector.reciprocal(out=inv_l[:], in_=sums[:, 0:1])
         pooled = consts.tile([P, FEATURES], F32)
         scale = consts.tile([P, 1], F32)
         for cols in halves:
             nc.vector.scalar_tensor_tensor(
-                out=pooled[:, cols], in0=bf_bc[:, cols], scalar=sum_c[:], in1=acc[:, cols], op0=ALU.mult, op1=ALU.add
+                out=pooled[:, cols], in0=bf_bc[:, cols], scalar=sums[:, 2:3], in1=acc[:, cols], op0=ALU.mult, op1=ALU.add
             )
             if cols == halves[0]:
                 nc.vector.tensor_scalar(
@@ -302,10 +302,8 @@ def tile_embed_update_pa_kernel(
             nc.vector.bn_stats(out=stats[:, i, :], in_=e_new[:, cols])
         mean_var = consts.tile([P, 2], F32)
         nc.vector.bn_aggr(out=mean_var[:], in_=stats[:].rearrange("p a b -> p (a b)"))
-        var_eps = consts.tile([P, 1], F32)
-        nc.vector.tensor_scalar_add(out=var_eps[:], in0=mean_var[:, 1:2], scalar1=LN_EPS)
         rstd = consts.tile([P, 1], F32)
-        nc.gpsimd.tensor_tensor(out=rstd[:], in0=var_eps[:], in1=minus_half[:], op=ALU.pow)
+        nc.scalar.activation(out=rstd[:], in_=mean_var[:, 1:2], func=ACT.Abs_reciprocal_sqrt, bias=ln_eps[:])
         centred = consts.tile([P, FEATURES], F32)
         for cols in halves:
             nc.vector.scalar_tensor_tensor(

@@ -74,18 +74,20 @@ def tile_embed_update_pa_kernel(
         gamma_bc = consts.tile([P, FEATURES], BF16)
         beta_bc = consts.tile([P, FEATURES], BF16)
 
-        nc.scalar.dma_start(out=b1_sb[:], in_=b1.rearrange("(p t) -> p t", t=PACK))
-        nc.scalar.dma_start(out=m_sb[:], in_=m.rearrange("b s l o -> (b s) (l o)"))
+        for g in range(IN_PASSES):
+            nc.sync.dma_start(
+                out=w1_raw[:, g, :], in_=W1_words[g].rearrange("p n t -> p (n t)").bitcast(I32)
+            )
         w1_rows = W1_scales.rearrange("g (q r) n -> r q g n", r=4)
         for r in range(4):
             nc.sync.dma_start(
                 out=planes[r:P:32, 0:IN_PASSES, :].bitcast(I32), in_=w1_rows[r].bitcast(I32)
             )
-        for g in range(IN_PASSES):
-            nc.sync.dma_start(
-                out=w1_raw[:, g, :], in_=W1_words[g].rearrange("p n t -> p (n t)").bitcast(I32)
-            )
-        for j in range(6):
+        load_x(0)
+        load_x(1)
+        nc.sync.dma_start(out=b1_sb[:], in_=b1.rearrange("(p t) -> p t", t=PACK))
+        nc.sync.dma_start(out=m_sb[:], in_=m.rearrange("b s l o -> (b s) (l o)"))
+        for j in range(2, 6):
             load_x(j)
         wf_rows = Wf_scales.rearrange("g (q r) n -> r q (g n)", r=4)
         for r in range(4):
@@ -118,12 +120,12 @@ def tile_embed_update_pa_kernel(
         w1_cols = consts.tile([P, IN_PASSES, PACK, P], I32, align_bytes=64)
         w1_planes = consts.tile([P, IN_PASSES, PACK, P], U8, align_bytes=64)
         raw_planes = planes[:, 0:IN_PASSES, :].rearrange("p g (m t) -> p g m t", t=PACK)
-        for t in range(PACK):
-            nc.vector.tensor_copy(out=w1_planes[:, :, t, :], in_=raw_planes[:, :, :, t])
         for g in range(IN_PASSES):
             nc.vector.tensor_copy(
                 out=w1_cols[:, g, :, :], in_=w1_raw[:, g, :].rearrange("p (m t) -> p t m", t=PACK)
             )
+        for t in range(PACK):
+            nc.vector.tensor_copy(out=w1_planes[:, :, t, :], in_=raw_planes[:, :, :, t])
 
         sig = consts.tile([P, LINKS], F32)
         terms = consts.tile([P, 3, LINKS], F32)

@@ -30,6 +30,7 @@ BLOCKS = LINKS // BLOCK_LINKS
 ROWS = BLOCK_LINKS * P
 HALF = 256
 RUN = 4
+WARM_UP = 6
 M1_LAG = 1
 M2_LAG = 2
 
@@ -53,6 +54,12 @@ def tile_embed_update_pa_kernel(
 
         def load_x(j):
             nc.sync.dma_start(out=x_sb[j][:], in_=x_dram[:, j, :])
+
+        zeros = consts.tile([P, CHANNELS], BF16)
+        nc.vector.memset(zeros[:], 0.0)
+        warm_ps = psum.tile([P, CHANNELS], F32, name="o_ps", bufs=4)
+        for i in range(WARM_UP):
+            nc.tensor.matmul(out=warm_ps[:], lhsT=zeros[:, 0:P], rhs=zeros[:], start=True, stop=True)
 
         planes = consts.tile([P, IN_PASSES + 1, HID], U8, align_bytes=64)
         nc.vector.memset(planes[:].bitcast(I32), 0)

@@ -30,7 +30,8 @@ BLOCKS = LINKS // BLOCK_LINKS
 ROWS = BLOCK_LINKS * P
 HALF = 256
 RUN = 4
-WARM_UP = 6
+WARM_UP = 4
+WARM_COLS = 256
 M1_LAG = 1
 M2_LAG = 2
 
@@ -55,14 +56,15 @@ def tile_embed_update_pa_kernel(
         def load_x(j):
             nc.sync.dma_start(out=x_sb[j][:], in_=x_dram[:, j, :])
 
-        zeros = consts.tile([P, CHANNELS], BF16)
+        planes = consts.tile([P, IN_PASSES + 1, HID], U8, align_bytes=64)
+        nc.vector.memset(planes[:].bitcast(I32), 0)
+        zeros = consts.tile([P, WARM_COLS], BF16)
         nc.vector.memset(zeros[:], 0.0)
         warm_ps = psum.tile([P, CHANNELS], F32, name="o_ps", bufs=4)
         for i in range(WARM_UP):
-            nc.tensor.matmul(out=warm_ps[:], lhsT=zeros[:, 0:P], rhs=zeros[:], start=True, stop=True)
-
-        planes = consts.tile([P, IN_PASSES + 1, HID], U8, align_bytes=64)
-        nc.vector.memset(planes[:].bitcast(I32), 0)
+            nc.tensor.matmul(
+                out=warm_ps[:, 0:WARM_COLS], lhsT=zeros[:, 0:P], rhs=zeros[:], start=True, stop=True
+            )
         ident = consts.tile([P, P], F32)
         make_identity(nc, ident[:])
         minus_half = consts.tile([P, 1], F32)
@@ -81,17 +83,17 @@ def tile_embed_update_pa_kernel(
         gamma_bc = consts.tile([P, FEATURES], BF16)
         beta_bc = consts.tile([P, FEATURES], BF16)
 
-        for g in range(IN_PASSES):
-            nc.sync.dma_start(
-                out=w1_raw[:, g, :], in_=W1_words[g].rearrange("p n t -> p (n t)").bitcast(I32)
-            )
+        load_x(0)
         w1_rows = W1_scales.rearrange("g (q r) n -> r q g n", r=4)
         for r in range(4):
             nc.sync.dma_start(
                 out=planes[r:P:32, 0:IN_PASSES, :].bitcast(I32), in_=w1_rows[r].bitcast(I32)
             )
-        load_x(0)
         load_x(1)
+        for g in range(IN_PASSES):
+            nc.sync.dma_start(
+                out=w1_raw[:, g, :], in_=W1_words[g].rearrange("p n t -> p (n t)").bitcast(I32)
+            )
         nc.sync.dma_start(out=b1_sb[:], in_=b1.rearrange("(p t) -> p t", t=PACK))
         nc.sync.dma_start(out=m_sb[:], in_=m.rearrange("b s l o -> (b s) (l o)"))
         for j in range(2, 6):
@@ -127,12 +129,11 @@ def tile_embed_update_pa_kernel(
         w1_cols = consts.tile([P, IN_PASSES, PACK, P], I32, align_bytes=64)
         w1_planes = consts.tile([P, IN_PASSES, PACK, P], U8, align_bytes=64)
         raw_planes = planes[:, 0:IN_PASSES, :].rearrange("p g (m t) -> p g m t", t=PACK)
-        for g in range(IN_PASSES):
-            nc.vector.tensor_copy(
-                out=w1_cols[:, g, :, :], in_=w1_raw[:, g, :].rearrange("p (m t) -> p t m", t=PACK)
-            )
+        raw_words = w1_raw[:].rearrange("p g (m t) -> p g m t", t=PACK)
         for t in range(PACK):
             nc.vector.tensor_copy(out=w1_planes[:, :, t, :], in_=raw_planes[:, :, :, t])
+        for t in range(PACK):
+            nc.vector.tensor_copy(out=w1_cols[:, :, t, :], in_=raw_words[:, :, :, t])
 
         sig = consts.tile([P, LINKS], F32)
         terms = consts.tile([P, 3, LINKS], F32)
@@ -241,6 +242,7 @@ def tile_embed_update_pa_kernel(
                     func=ACT.Sigmoid,
                     bias=bf_bc[:, FEATURES:CHANNELS],
                 )
+            for j in links_of(blk):
                 nc.scalar.activation(
                     out=terms[:, 2, j : j + 1],
                     in_=sig[:, j : j + 1],

@@ -28,6 +28,7 @@ LINK_EPS = 1e-8
 BLOCK_LINKS = 2
 BLOCKS = LINKS // BLOCK_LINKS
 ROWS = BLOCK_LINKS * P
+EARLY = LINKS - BLOCK_LINKS
 HALF = 256
 RUN = 4
 WARM_UP = 4
@@ -72,6 +73,11 @@ def tile_embed_update_pa_kernel(
         ln_eps = consts.tile([P, 1], F32)
         nc.gpsimd.tensor_scalar(
             out=ln_eps[:], in0=minus_half[:], scalar1=0.0, scalar2=LN_EPS, op0=ALU.mult, op1=ALU.add
+        )
+
+        link_eps = consts.tile([P, 1], F32)
+        nc.gpsimd.tensor_scalar(
+            out=link_eps[:], in0=minus_half[:], scalar1=0.0, scalar2=LINK_EPS, op0=ALU.mult, op1=ALU.add
         )
 
         w1_raw = consts.tile([P, IN_PASSES, HID], I32)
@@ -125,6 +131,10 @@ def tile_embed_update_pa_kernel(
         nc.gpsimd.tensor_scalar(
             out=m_eps[:], in0=m_sb[:], scalar1=LINK_EPS, scalar2=0.0, op0=ALU.mult, op1=ALU.add
         )
+        m_late = consts.tile([P, BLOCK_LINKS], F32)
+        nc.gpsimd.tensor_scalar(
+            out=m_late[:], in0=m_sb[:, EARLY:LINKS], scalar1=1.0, scalar2=0.0, op0=ALU.mult, op1=ALU.add
+        )
 
         w1_cols = consts.tile([P, IN_PASSES, PACK, P], I32, align_bytes=64)
         w1_planes = consts.tile([P, IN_PASSES, PACK, P], U8, align_bytes=64)
@@ -132,12 +142,22 @@ def tile_embed_update_pa_kernel(
         raw_words = w1_raw[:].rearrange("p g (m t) -> p g m t", t=PACK)
         for t in range(PACK):
             nc.vector.tensor_copy(out=w1_planes[:, :, t, :], in_=raw_planes[:, :, :, t])
-        for t in range(PACK):
-            nc.vector.tensor_copy(out=w1_cols[:, :, t, :], in_=raw_words[:, :, :, t])
+
+        def sort_words(slots):
+            for t in slots:
+                nc.vector.tensor_copy(out=w1_cols[:, :, t, :], in_=raw_words[:, :, :, t])
+
 
         sig = consts.tile([P, LINKS], F32)
         terms = consts.tile([P, 3, LINKS], F32)
         acc = consts.tile([P, FEATURES], F32)
+        nc.gpsimd.memset(sig[:, EARLY:LINKS], 0.0)
+        nc.gpsimd.tensor_scalar(
+            out=terms[:, 2, EARLY:LINKS], in0=m_eps[:, EARLY:LINKS], scalar1=1.0, scalar2=0.0, op0=ALU.mult, op1=ALU.add
+        )
+        g_all = consts.tile([P, LINKS], F32)
+        sums = consts.tile([P, 1 + BLOCK_LINKS, 3], F32)
+        late = consts.tile([P, 4, BLOCK_LINKS], F32)
         xt_ps, x_grouped, x_codes, x_scales = {}, {}, {}, {}
         h_ps, h_slots, h_grouped, h_codes, h_scales, o_ps = {}, {}, {}, {}, {}, {}
 
@@ -222,6 +242,12 @@ def tile_embed_update_pa_kernel(
                 in_=h_grouped[blk][:].rearrange("p r t -> p (r t)"),
             )
 
+        def sigmoid_of(j):
+            return sig[:, j : j + 1] if j < EARLY else late[:, 0, j - EARLY : j - EARLY + 1]
+
+        def weight_of(j):
+            return terms[:, 2, j : j + 1] if j < EARLY else late[:, 1, j - EARLY : j - EARLY + 1]
+
         def second_matmul(blk):
             for i, j in enumerate(links_of(blk)):
                 tokens = slice(i * P, (i + 1) * P)
@@ -237,15 +263,15 @@ def tile_embed_update_pa_kernel(
                 )
             for j in links_of(blk):
                 nc.scalar.activation(
-                    out=sig[:, j : j + 1],
+                    out=sigmoid_of(j),
                     in_=o_ps[j][:, FEATURES:CHANNELS],
                     func=ACT.Sigmoid,
                     bias=bf_bc[:, FEATURES:CHANNELS],
                 )
             for j in links_of(blk):
                 nc.scalar.activation(
-                    out=terms[:, 2, j : j + 1],
-                    in_=sig[:, j : j + 1],
+                    out=weight_of(j),
+                    in_=sigmoid_of(j),
                     func=ACT.Identity,
                     scale=m_sq[:, j : j + 1],
                     bias=m_eps[:, j : j + 1],
@@ -253,12 +279,12 @@ def tile_embed_update_pa_kernel(
 
         def pool_columns(j, cols):
             if j == 0:
-                nc.vector.tensor_scalar_mul(out=acc[:, cols], in0=o_ps[j][:, cols], scalar1=terms[:, 2, j : j + 1])
+                nc.vector.tensor_scalar_mul(out=acc[:, cols], in0=o_ps[j][:, cols], scalar1=weight_of(j))
             else:
                 nc.vector.scalar_tensor_tensor(
                     out=acc[:, cols],
                     in0=o_ps[j][:, cols],
-                    scalar=terms[:, 2, j : j + 1],
+                    scalar=weight_of(j),
                     in1=acc[:, cols],
                     op0=ALU.mult,
                     op1=ALU.add,
@@ -268,7 +294,11 @@ def tile_embed_update_pa_kernel(
             if 0 <= blk < BLOCKS - 1:
                 pool_columns(links_of(blk)[i], slice(0, FEATURES))
 
-        for step in range(BLOCKS + M2_LAG):
+        sort_words(range(1))
+        transpose_x(0)
+        quantise_x(0)
+        sort_words(range(1, PACK))
+        for step in range(1, BLOCKS + M2_LAG):
             transpose_x(step)
             first_matmul(step - M1_LAG)
             second_matmul(step - M2_LAG)
@@ -279,28 +309,53 @@ def tile_embed_update_pa_kernel(
             pool_link(step - M2_LAG, 1)
 
         halves = (slice(0, HALF), slice(HALF, FEATURES))
-        nc.scalar.activation(out=table_warm[:], in_=ln_eps[:], func=ACT.Abs_reciprocal_sqrt)
-        g_all = consts.tile([P, LINKS], F32)
-        sums = consts.tile([P, 3], F32)
-        pool_columns(LINKS - 2, halves[0])
         nc.vector.tensor_tensor(out=g_all[:], in0=sig[:], in1=m_sb[:], op=ALU.mult)
-        pool_columns(LINKS - 2, halves[1])
         nc.vector.tensor_scalar_add(out=terms[:, 0, :], in0=g_all[:], scalar1=LINK_EPS)
-        pool_columns(LINKS - 1, halves[0])
         nc.vector.tensor_tensor(out=terms[:, 1, :], in0=terms[:, 0, :], in1=g_all[:], op=ALU.mult)
-        pool_columns(LINKS - 1, halves[1])
-        nc.vector.tensor_reduce(out=sums[:], in_=terms[:], axis=AXIS.X, op=ALU.add)
+        nc.vector.tensor_reduce(out=sums[:, 0, :], in_=terms[:], axis=AXIS.X, op=ALU.add)
+        for i in range(BLOCK_LINKS):
+            j = EARLY + i
+            m_j = m_late[:, i : i + 1]
+            nc.scalar.activation(
+                out=sums[:, i + 1, 0:1], in_=sigmoid_of(j), func=ACT.Identity, scale=m_j, bias=sums[:, i, 0:1]
+            )
+            nc.scalar.activation(out=late[:, 2, i : i + 1], in_=sigmoid_of(j), func=ACT.Copy, scale=m_j)
+            nc.scalar.activation(
+                out=late[:, 3, i : i + 1], in_=sigmoid_of(j), func=ACT.Identity, scale=m_j, bias=link_eps[:]
+            )
+        for i in range(BLOCK_LINKS):
+            j = EARLY + i
+            nc.scalar.activation(
+                out=sums[:, i + 1, 1:2],
+                in_=late[:, 3, i : i + 1],
+                func=ACT.Identity,
+                scale=late[:, 2, i : i + 1],
+                bias=sums[:, i, 1:2],
+            )
+            nc.scalar.activation(
+                out=sums[:, i + 1, 2:3],
+                in_=sigmoid_of(j),
+                func=ACT.Identity,
+                scale=m_sq[:, j : j + 1],
+                bias=sums[:, i, 2:3],
+            )
+        totals = sums[:, BLOCK_LINKS, :]
+        nc.scalar.activation(out=table_warm[:], in_=ln_eps[:], func=ACT.Abs_reciprocal_sqrt)
         inv_l = consts.tile([P, 1], F32)
-        nc.vector.reciprocal(out=inv_l[:], in_=sums[:, 0:1])
+        pool_columns(LINKS - 2, halves[0])
+        pool_columns(LINKS - 2, halves[1])
+        pool_columns(LINKS - 1, halves[0])
+        nc.vector.reciprocal(out=inv_l[:], in_=totals[:, 0:1])
+        pool_columns(LINKS - 1, halves[1])
         pooled = consts.tile([P, FEATURES], F32)
         scale = consts.tile([P, 1], F32)
         for cols in halves:
             nc.vector.scalar_tensor_tensor(
-                out=pooled[:, cols], in0=bf_bc[:, cols], scalar=sums[:, 2:3], in1=acc[:, cols], op0=ALU.mult, op1=ALU.add
+                out=pooled[:, cols], in0=bf_bc[:, cols], scalar=totals[:, 2:3], in1=acc[:, cols], op0=ALU.mult, op1=ALU.add
             )
             if cols == halves[0]:
                 nc.vector.tensor_scalar(
-                    out=scale[:], in0=sums[:, 1:2], scalar1=inv_l[:], scalar2=inv_l[:], op0=ALU.mult, op1=ALU.mult
+                    out=scale[:], in0=totals[:, 1:2], scalar1=inv_l[:], scalar2=inv_l[:], op0=ALU.mult, op1=ALU.mult
                 )
         e_new = consts.tile([P, FEATURES], F32)
         for cols in halves:

@@ -32,7 +32,7 @@ EARLY = LINKS - BLOCK_LINKS
 HALF = 256
 RUN = 4
 WARM_UP = 4
-WARM_COLS = 256
+WARM_BEHIND = {0: 1, 1: 3, 2: 1}
 M1_LAG = 1
 M2_LAG = 2
 
@@ -58,14 +58,16 @@ def tile_embed_update_pa_kernel(
             nc.sync.dma_start(out=x_sb[j][:], in_=x_dram[:, j, :])
 
         planes = consts.tile([P, IN_PASSES + 1, HID], U8, align_bytes=64)
-        nc.vector.memset(planes[:].bitcast(I32), 0)
-        zeros = consts.tile([P, WARM_COLS], BF16)
+        nc.gpsimd.memset(planes[:].bitcast(F32), 0.0)
+        zeros = consts.tile([P, CHANNELS], BF16)
         nc.vector.memset(zeros[:], 0.0)
         warm_ps = psum.tile([P, CHANNELS], F32, name="o_ps", bufs=4)
-        for i in range(WARM_UP):
-            nc.tensor.matmul(
-                out=warm_ps[:, 0:WARM_COLS], lhsT=zeros[:, 0:P], rhs=zeros[:], start=True, stop=True
-            )
+
+        def warm_up(times):
+            for i in range(times):
+                nc.tensor.matmul(out=warm_ps[:], lhsT=zeros[:, 0:P], rhs=zeros[:], start=True, stop=True)
+
+        warm_up(WARM_UP)
         ident = consts.tile([P, P], F32)
         make_identity(nc, ident[:])
         minus_half = consts.tile([P, 1], F32)
@@ -100,10 +102,12 @@ def tile_embed_update_pa_kernel(
             nc.sync.dma_start(
                 out=w1_raw[:, g, :], in_=W1_words[g].rearrange("p n t -> p (n t)").bitcast(I32)
             )
+        load_x(2)
+        load_x(3)
         nc.sync.dma_start(out=b1_sb[:], in_=b1.rearrange("(p t) -> p t", t=PACK))
         nc.sync.dma_start(out=m_sb[:], in_=m.rearrange("b s l o -> (b s) (l o)"))
-        for j in range(2, 6):
-            load_x(j)
+        load_x(4)
+        load_x(5)
         wf_rows = Wf_scales.rearrange("g (q r) n -> r q (g n)", r=4)
         for r in range(4):
             nc.sync.dma_start(
@@ -179,6 +183,7 @@ def tile_embed_update_pa_kernel(
                         nc.tensor.transpose(
                             xt_ps[j][:, g, u, :], words[:, first : (g + 1) * (K_PASS // 2) : 2], ident[:]
                         )
+                warm_up(WARM_BEHIND.get(j, 0))
                 nc.scalar.copy(
                     out=x_grouped[blk][:, :, i * P : (i + 1) * P, :].bitcast(F32),
                     in_=xt_ps[j][:].rearrange("p g u r -> p g r u"),
@@ -314,30 +319,37 @@ def tile_embed_update_pa_kernel(
         nc.vector.tensor_tensor(out=terms[:, 1, :], in0=terms[:, 0, :], in1=g_all[:], op=ALU.mult)
         nc.vector.tensor_reduce(out=sums[:, 0, :], in_=terms[:], axis=AXIS.X, op=ALU.add)
         for i in range(BLOCK_LINKS):
-            j = EARLY + i
-            m_j = m_late[:, i : i + 1]
             nc.scalar.activation(
-                out=sums[:, i + 1, 0:1], in_=sigmoid_of(j), func=ACT.Identity, scale=m_j, bias=sums[:, i, 0:1]
+                out=sums[:, i + 1, 0:1],
+                in_=sigmoid_of(EARLY + i),
+                func=ACT.Identity,
+                scale=m_late[:, i : i + 1],
+                bias=sums[:, i, 0:1],
             )
-            nc.scalar.activation(out=late[:, 2, i : i + 1], in_=sigmoid_of(j), func=ACT.Copy, scale=m_j)
             nc.scalar.activation(
-                out=late[:, 3, i : i + 1], in_=sigmoid_of(j), func=ACT.Identity, scale=m_j, bias=link_eps[:]
+                out=sums[:, i + 1, 2:3],
+                in_=sigmoid_of(EARLY + i),
+                func=ACT.Identity,
+                scale=m_sq[:, EARLY + i : EARLY + i + 1],
+                bias=sums[:, i, 2:3],
+            )
+            nc.scalar.activation(
+                out=late[:, 2, i : i + 1], in_=sigmoid_of(EARLY + i), func=ACT.Copy, scale=m_late[:, i : i + 1]
+            )
+            nc.scalar.activation(
+                out=late[:, 3, i : i + 1],
+                in_=sigmoid_of(EARLY + i),
+                func=ACT.Identity,
+                scale=m_late[:, i : i + 1],
+                bias=link_eps[:],
             )
         for i in range(BLOCK_LINKS):
-            j = EARLY + i
             nc.scalar.activation(
                 out=sums[:, i + 1, 1:2],
                 in_=late[:, 3, i : i + 1],
                 func=ACT.Identity,
                 scale=late[:, 2, i : i + 1],
                 bias=sums[:, i, 1:2],
-            )
-            nc.scalar.activation(
-                out=sums[:, i + 1, 2:3],
-                in_=sigmoid_of(j),
-                func=ACT.Identity,
-                scale=m_sq[:, j : j + 1],
-                bias=sums[:, i, 2:3],
             )
         totals = sums[:, BLOCK_LINKS, :]
         nc.scalar.activation(out=table_warm[:], in_=ln_eps[:], func=ACT.Abs_reciprocal_sqrt)

@@ -31,8 +31,7 @@ ROWS = BLOCK_LINKS * P
 EARLY = LINKS - BLOCK_LINKS
 HALF = 256
 RUN = 4
-WARM_UP = 4
-WARM_BEHIND = {0: 1, 1: 3, 2: 1}
+WARM_UP = 3
 M1_LAG = 1
 M2_LAG = 2
 
@@ -62,12 +61,8 @@ def tile_embed_update_pa_kernel(
         zeros = consts.tile([P, CHANNELS], BF16)
         nc.vector.memset(zeros[:], 0.0)
         warm_ps = psum.tile([P, CHANNELS], F32, name="o_ps", bufs=4)
-
-        def warm_up(times):
-            for i in range(times):
-                nc.tensor.matmul(out=warm_ps[:], lhsT=zeros[:, 0:P], rhs=zeros[:], start=True, stop=True)
-
-        warm_up(WARM_UP)
+        for i in range(WARM_UP):
+            nc.tensor.matmul(out=warm_ps[:], lhsT=zeros[:, 0:P], rhs=zeros[:], start=True, stop=True)
         ident = consts.tile([P, P], F32)
         make_identity(nc, ident[:])
         minus_half = consts.tile([P, 1], F32)
@@ -183,7 +178,6 @@ def tile_embed_update_pa_kernel(
                         nc.tensor.transpose(
                             xt_ps[j][:, g, u, :], words[:, first : (g + 1) * (K_PASS // 2) : 2], ident[:]
                         )
-                warm_up(WARM_BEHIND.get(j, 0))
                 nc.scalar.copy(
                     out=x_grouped[blk][:, :, i * P : (i + 1) * P, :].bitcast(F32),
                     in_=xt_ps[j][:].rearrange("p g u r -> p g r u"),

@@ -31,7 +31,8 @@ ROWS = BLOCK_LINKS * P
 EARLY = LINKS - BLOCK_LINKS
 HALF = 256
 RUN = 4
-WARM_UP = 3
+WARM_UP = 6
+WARM_COLS = 256
 M1_LAG = 1
 M2_LAG = 2
 
@@ -49,20 +50,27 @@ def tile_embed_update_pa_kernel(
         stack.enter_context(tc.manual_schedule())
 
         x_dram = net_in.rearrange("b s l k -> (b s) l k")
-        x_sb = []
-        for j in range(LINKS):
-            x_sb.append(consts.tile([P, IN], BF16, name="x%d" % j))
+        x_sb, x_pairs = [], []
+        for j in range(0, LINKS, 2):
+            pair = consts.tile([P, 2, IN], BF16, name="x%d" % j)
+            x_sb.extend([pair[:, 0, :], pair[:, 1, :]])
+            x_pairs.append(pair)
 
         def load_x(j):
-            nc.sync.dma_start(out=x_sb[j][:], in_=x_dram[:, j, :])
+            nc.sync.dma_start(out=x_sb[j], in_=x_dram[:, j, :])
+
+        def load_pair(j):
+            nc.sync.dma_start(out=x_pairs[j // 2][:], in_=x_dram[:, j : j + 2, :])
 
         planes = consts.tile([P, IN_PASSES + 1, HID], U8, align_bytes=64)
-        nc.gpsimd.memset(planes[:].bitcast(F32), 0.0)
-        zeros = consts.tile([P, CHANNELS], BF16)
-        nc.vector.memset(zeros[:], 0.0)
+        nc.vector.memset(planes[:].bitcast(I32), 0)
+        zeros = consts.tile([P, WARM_COLS], BF16)
+        nc.gpsimd.memset(zeros[:], 0.0)
         warm_ps = psum.tile([P, CHANNELS], F32, name="o_ps", bufs=4)
         for i in range(WARM_UP):
-            nc.tensor.matmul(out=warm_ps[:], lhsT=zeros[:, 0:P], rhs=zeros[:], start=True, stop=True)
+            nc.tensor.matmul(
+                out=warm_ps[:, 0:WARM_COLS], lhsT=zeros[:, 0:P], rhs=zeros[:], start=True, stop=True
+            )
         ident = consts.tile([P, P], F32)
         make_identity(nc, ident[:])
         minus_half = consts.tile([P, 1], F32)
@@ -86,23 +94,20 @@ def tile_embed_update_pa_kernel(
         gamma_bc = consts.tile([P, FEATURES], BF16)
         beta_bc = consts.tile([P, FEATURES], BF16)
 
+        nc.gpsimd.dma_start(out=b1_sb[:], in_=b1.rearrange("(p t) -> p t", t=PACK))
+        nc.gpsimd.dma_start(out=m_sb[:], in_=m.rearrange("b s l o -> (b s) (l o)"))
         load_x(0)
+        load_x(1)
         w1_rows = W1_scales.rearrange("g (q r) n -> r q g n", r=4)
         for r in range(4):
             nc.sync.dma_start(
                 out=planes[r:P:32, 0:IN_PASSES, :].bitcast(I32), in_=w1_rows[r].bitcast(I32)
             )
-        load_x(1)
-        for g in range(IN_PASSES):
-            nc.sync.dma_start(
-                out=w1_raw[:, g, :], in_=W1_words[g].rearrange("p n t -> p (n t)").bitcast(I32)
-            )
-        load_x(2)
-        load_x(3)
-        nc.sync.dma_start(out=b1_sb[:], in_=b1.rearrange("(p t) -> p t", t=PACK))
-        nc.sync.dma_start(out=m_sb[:], in_=m.rearrange("b s l o -> (b s) (l o)"))
-        load_x(4)
-        load_x(5)
+        nc.sync.dma_start(
+            out=w1_raw[:], in_=W1_words.rearrange("g p n t -> p g (n t)").bitcast(I32)
+        )
+        load_pair(2)
+        load_pair(4)
         wf_rows = Wf_scales.rearrange("g (q r) n -> r q (g n)", r=4)
         for r in range(4):
             nc.sync.dma_start(
@@ -112,11 +117,10 @@ def tile_embed_update_pa_kernel(
             out=wf_words[:].bitcast(I32),
             in_=Wf_words.rearrange("g p n t -> p (g n t)").bitcast(I32),
         )
-        load_x(6)
-        load_x(7)
+        load_pair(6)
         nc.sync.dma_start(out=bf_bc[:], in_=b_f.partition_broadcast(P))
-        for j in range(8, LINKS):
-            load_x(j)
+        for j in range(8, LINKS, 2):
+            load_pair(j)
         nc.sync.dma_start(out=emb_sb[:], in_=embeds.rearrange("b s c -> (b s) c"))
         nc.sync.dma_start(out=gamma_bc[:], in_=gamma.partition_broadcast(P))
         nc.sync.dma_start(out=beta_bc[:], in_=beta.partition_broadcast(P))
@@ -170,7 +174,7 @@ def tile_embed_update_pa_kernel(
                 return
             x_grouped[blk] = work.tile([P, IN_PASSES, ROWS, PACK], BF16, name="x_grouped", align_bytes=64)
             for i, j in enumerate(links_of(blk)):
-                words = x_sb[j][:].bitcast(F32)
+                words = x_sb[j].bitcast(F32)
                 xt_ps[j] = psum.tile([P, IN_PASSES, 2, P], F32, name="xt_ps")
                 for g in range(IN_PASSES):
                     for u in range(2):

@@ -30,9 +30,9 @@ BLOCKS = LINKS // BLOCK_LINKS
 ROWS = BLOCK_LINKS * P
 EARLY = LINKS - BLOCK_LINKS
 HALF = 256
+GATE_COLS = 64
 RUN = 4
-WARM_UP = 6
-WARM_COLS = 256
+WARM_UP = 3
 M1_LAG = 1
 M2_LAG = 2
 
@@ -64,13 +64,11 @@ def tile_embed_update_pa_kernel(
 
         planes = consts.tile([P, IN_PASSES + 1, HID], U8, align_bytes=64)
         nc.vector.memset(planes[:].bitcast(I32), 0)
-        zeros = consts.tile([P, WARM_COLS], BF16)
+        zeros = consts.tile([P, CHANNELS], BF16)
         nc.gpsimd.memset(zeros[:], 0.0)
         warm_ps = psum.tile([P, CHANNELS], F32, name="o_ps", bufs=4)
         for i in range(WARM_UP):
-            nc.tensor.matmul(
-                out=warm_ps[:, 0:WARM_COLS], lhsT=zeros[:, 0:P], rhs=zeros[:], start=True, stop=True
-            )
+            nc.tensor.matmul(out=warm_ps[:], lhsT=zeros[:, 0:P], rhs=zeros[:], start=True, stop=True)
         ident = consts.tile([P, P], F32)
         make_identity(nc, ident[:])
         minus_half = consts.tile([P, 1], F32)
@@ -251,23 +249,32 @@ def tile_embed_update_pa_kernel(
         def weight_of(j):
             return terms[:, 2, j : j + 1] if j < EARLY else late[:, 1, j - EARLY : j - EARLY + 1]
 
+        def second_pass(blk, i, out, cols):
+            tokens = slice(i * P, (i + 1) * P)
+            nc.tensor.matmul_mx(
+                out=out,
+                lhsT=h_codes[blk][:, tokens].bitcast(FP8X4),
+                lhsT_scale=h_scales[blk][:, tokens],
+                rhs=wf_words[:, cols].bitcast(FP8X4),
+                rhs_scale=planes[:, IN_PASSES, cols],
+                start=True,
+                stop=True,
+            )
+
         def second_matmul(blk):
+            gate = {}
+            if blk == BLOCKS - 1:
+                for i, j in enumerate(links_of(blk)):
+                    gate_ps = psum.tile([P, GATE_COLS], F32, name="xt_ps")
+                    second_pass(blk, i, gate_ps[:], slice(CHANNELS - GATE_COLS, CHANNELS))
+                    gate[j] = gate_ps[:, GATE_COLS - 1 : GATE_COLS]
             for i, j in enumerate(links_of(blk)):
-                tokens = slice(i * P, (i + 1) * P)
                 o_ps[j] = psum.tile([P, CHANNELS], F32, name="o_ps", bufs=4)
-                nc.tensor.matmul_mx(
-                    out=o_ps[j][:],
-                    lhsT=h_codes[blk][:, tokens].bitcast(FP8X4),
-                    lhsT_scale=h_scales[blk][:, tokens],
-                    rhs=wf_words[:].bitcast(FP8X4),
-                    rhs_scale=planes[:, IN_PASSES, :],
-                    start=True,
-                    stop=True,
-                )
+                second_pass(blk, i, o_ps[j][:], slice(0, CHANNELS))
             for j in links_of(blk):
                 nc.scalar.activation(
                     out=sigmoid_of(j),
-                    in_=o_ps[j][:, FEATURES:CHANNELS],
+                    in_=gate.get(j, o_ps[j][:, FEATURES:CHANNELS]),
                     func=ACT.Sigmoid,
                     bias=bf_bc[:, FEATURES:CHANNELS],
                 )
@@ -302,13 +309,18 @@ def tile_embed_update_pa_kernel(
         quantise_x(0)
         sort_words(range(1, PACK))
         for step in range(1, BLOCKS + M2_LAG):
-            transpose_x(step)
+            if step < BLOCKS - 1:
+                transpose_x(step)
             first_matmul(step - M1_LAG)
             second_matmul(step - M2_LAG)
-            quantise_x(step)
+            if step < BLOCKS - 1:
+                quantise_x(step)
             group_h(step - M1_LAG)
             pool_link(step - M2_LAG, 0)
             quantise_h(step - M1_LAG)
+            if step == BLOCKS - 2:
+                transpose_x(step + 1)
+                quantise_x(step + 1)
             pool_link(step - M2_LAG, 1)
 
         halves = (slice(0, HALF), slice(HALF, FEATURES))

@@ -94,8 +94,8 @@ def tile_embed_update_pa_kernel(
 
         nc.gpsimd.dma_start(out=b1_sb[:], in_=b1.rearrange("(p t) -> p t", t=PACK))
         nc.gpsimd.dma_start(out=m_sb[:], in_=m.rearrange("b s l o -> (b s) (l o)"))
-        load_x(0)
-        load_x(1)
+        for j in range(3):
+            load_x(j)
         w1_rows = W1_scales.rearrange("g (q r) n -> r q g n", r=4)
         for r in range(4):
             nc.sync.dma_start(
@@ -104,7 +104,7 @@ def tile_embed_update_pa_kernel(
         nc.sync.dma_start(
             out=w1_raw[:], in_=W1_words.rearrange("g p n t -> p g (n t)").bitcast(I32)
         )
-        load_pair(2)
+        load_x(3)
         load_pair(4)
         wf_rows = Wf_scales.rearrange("g (q r) n -> r q (g n)", r=4)
         for r in range(4):
@@ -301,14 +301,14 @@ def tile_embed_update_pa_kernel(
                 )
 
         def pool_link(blk, i):
-            if 0 <= blk < BLOCKS - 1:
+            if 0 <= blk:
                 pool_columns(links_of(blk)[i], slice(0, FEATURES))
 
         sort_words(range(1))
         transpose_x(0)
         quantise_x(0)
         sort_words(range(1, PACK))
-        for step in range(1, BLOCKS + M2_LAG):
+        for step in range(1, BLOCKS):
             if step < BLOCKS - 1:
                 transpose_x(step)
             first_matmul(step - M1_LAG)
@@ -324,25 +324,22 @@ def tile_embed_update_pa_kernel(
             pool_link(step - M2_LAG, 1)
 
         halves = (slice(0, HALF), slice(HALF, FEATURES))
+        last = BLOCKS - 1
+        before = links_of(last - 1)
+        first_matmul(last)
+        second_matmul(last - 1)
+        group_h(last)
+        pool_columns(before[0], halves[0])
+        quantise_h(last)
+        second_matmul(last)
         nc.vector.tensor_tensor(out=g_all[:], in0=sig[:], in1=m_sb[:], op=ALU.mult)
+        pool_columns(before[0], halves[1])
         nc.vector.tensor_scalar_add(out=terms[:, 0, :], in0=g_all[:], scalar1=LINK_EPS)
+        pool_columns(before[1], halves[0])
         nc.vector.tensor_tensor(out=terms[:, 1, :], in0=terms[:, 0, :], in1=g_all[:], op=ALU.mult)
+        pool_columns(before[1], halves[1])
         nc.vector.tensor_reduce(out=sums[:, 0, :], in_=terms[:], axis=AXIS.X, op=ALU.add)
         for i in range(BLOCK_LINKS):
-            nc.scalar.activation(
-                out=sums[:, i + 1, 0:1],
-                in_=sigmoid_of(EARLY + i),
-                func=ACT.Identity,
-                scale=m_late[:, i : i + 1],
-                bias=sums[:, i, 0:1],
-            )
-            nc.scalar.activation(
-                out=sums[:, i + 1, 2:3],
-                in_=sigmoid_of(EARLY + i),
-                func=ACT.Identity,
-                scale=m_sq[:, EARLY + i : EARLY + i + 1],
-                bias=sums[:, i, 2:3],
-            )
             nc.scalar.activation(
                 out=late[:, 2, i : i + 1], in_=sigmoid_of(EARLY + i), func=ACT.Copy, scale=m_late[:, i : i + 1]
             )
@@ -354,21 +351,28 @@ def tile_embed_update_pa_kernel(
                 bias=link_eps[:],
             )
         for i in range(BLOCK_LINKS):
-            nc.scalar.activation(
-                out=sums[:, i + 1, 1:2],
-                in_=late[:, 3, i : i + 1],
-                func=ACT.Identity,
-                scale=late[:, 2, i : i + 1],
-                bias=sums[:, i, 1:2],
-            )
+            for s, (factor, part) in enumerate(
+                (
+                    (m_late[:, i : i + 1], sigmoid_of(EARLY + i)),
+                    (late[:, 2, i : i + 1], late[:, 3, i : i + 1]),
+                    (m_sq[:, EARLY + i : EARLY + i + 1], sigmoid_of(EARLY + i)),
+                )
+            ):
+                nc.scalar.activation(
+                    out=sums[:, i + 1, s : s + 1],
+                    in_=part,
+                    func=ACT.Identity,
+                    scale=factor,
+                    bias=sums[:, i, s : s + 1],
+                )
         totals = sums[:, BLOCK_LINKS, :]
         nc.scalar.activation(out=table_warm[:], in_=ln_eps[:], func=ACT.Abs_reciprocal_sqrt)
         inv_l = consts.tile([P, 1], F32)
-        pool_columns(LINKS - 2, halves[0])
-        pool_columns(LINKS - 2, halves[1])
-        pool_columns(LINKS - 1, halves[0])
+        pool_columns(EARLY, halves[0])
+        pool_columns(EARLY, halves[1])
+        pool_columns(EARLY + 1, halves[0])
         nc.vector.reciprocal(out=inv_l[:], in_=totals[:, 0:1])
-        pool_columns(LINKS - 1, halves[1])
+        pool_columns(EARLY + 1, halves[1])
         pooled = consts.tile([P, FEATURES], F32)
         scale = consts.tile([P, 1], F32)
         for cols in halves:

@@ -32,6 +32,7 @@ EARLY = LINKS - BLOCK_LINKS
 HALF = 256
 GATE_COLS = 64
 RUN = 4
+LOADS = (1, 2, 1, 2, 2, 2, 2, 2, 2)
 WARM_UP = 3
 M1_LAG = 1
 M2_LAG = 2
@@ -50,17 +51,14 @@ def tile_embed_update_pa_kernel(
         stack.enter_context(tc.manual_schedule())
 
         x_dram = net_in.rearrange("b s l k -> (b s) l k")
-        x_sb, x_pairs = [], []
-        for j in range(0, LINKS, 2):
-            pair = consts.tile([P, 2, IN], BF16, name="x%d" % j)
-            x_sb.extend([pair[:, 0, :], pair[:, 1, :]])
-            x_pairs.append(pair)
+        x_sb, x_tiles = [], []
+        for n in LOADS:
+            x_tiles.append(consts.tile([P, n, IN], BF16, name="x%d" % len(x_sb)))
+            x_sb.extend([x_tiles[-1][:, i, :] for i in range(n)])
 
-        def load_x(j):
-            nc.sync.dma_start(out=x_sb[j], in_=x_dram[:, j, :])
-
-        def load_pair(j):
-            nc.sync.dma_start(out=x_pairs[j // 2][:], in_=x_dram[:, j : j + 2, :])
+        def load_x(i):
+            first = sum(LOADS[:i])
+            nc.sync.dma_start(out=x_tiles[i][:], in_=x_dram[:, first : first + LOADS[i], :])
 
         planes = consts.tile([P, IN_PASSES + 1, HID], U8, align_bytes=64)
         nc.vector.memset(planes[:].bitcast(I32), 0)
@@ -94,8 +92,8 @@ def tile_embed_update_pa_kernel(
 
         nc.gpsimd.dma_start(out=b1_sb[:], in_=b1.rearrange("(p t) -> p t", t=PACK))
         nc.gpsimd.dma_start(out=m_sb[:], in_=m.rearrange("b s l o -> (b s) (l o)"))
-        for j in range(3):
-            load_x(j)
+        load_x(0)
+        load_x(1)
         w1_rows = W1_scales.rearrange("g (q r) n -> r q g n", r=4)
         for r in range(4):
             nc.sync.dma_start(
@@ -104,8 +102,8 @@ def tile_embed_update_pa_kernel(
         nc.sync.dma_start(
             out=w1_raw[:], in_=W1_words.rearrange("g p n t -> p g (n t)").bitcast(I32)
         )
+        load_x(2)
         load_x(3)
-        load_pair(4)
         wf_rows = Wf_scales.rearrange("g (q r) n -> r q (g n)", r=4)
         for r in range(4):
             nc.sync.dma_start(
@@ -115,10 +113,10 @@ def tile_embed_update_pa_kernel(
             out=wf_words[:].bitcast(I32),
             in_=Wf_words.rearrange("g p n t -> p (g n t)").bitcast(I32),
         )
-        load_pair(6)
+        load_x(4)
         nc.sync.dma_start(out=bf_bc[:], in_=b_f.partition_broadcast(P))
-        for j in range(8, LINKS, 2):
-            load_pair(j)
+        for i in range(5, len(LOADS)):
+            load_x(i)
         nc.sync.dma_start(out=emb_sb[:], in_=embeds.rearrange("b s c -> (b s) c"))
         nc.sync.dma_start(out=gamma_bc[:], in_=gamma.partition_broadcast(P))
         nc.sync.dma_start(out=beta_bc[:], in_=beta.partition_broadcast(P))

@@ -85,13 +85,15 @@ def tile_embed_update_pa_kernel(
         wf_words = consts.tile([P, CHANNELS], U32, align_bytes=64)
         m_sb = consts.tile([P, LINKS], BF16)
         b1_sb = consts.tile([P, PACK], BF16)
-        bf_bc = consts.tile([P, CHANNELS], BF16)
+        bf_bc = consts.tile([P, FEATURES], BF16)
+        bf_gate = consts.tile([P, 1], BF16)
         emb_sb = consts.tile([P, FEATURES], BF16)
         gamma_bc = consts.tile([P, FEATURES], BF16)
         beta_bc = consts.tile([P, FEATURES], BF16)
 
         nc.gpsimd.dma_start(out=b1_sb[:], in_=b1.rearrange("(p t) -> p t", t=PACK))
         nc.gpsimd.dma_start(out=m_sb[:], in_=m.rearrange("b s l o -> (b s) (l o)"))
+        nc.gpsimd.dma_start(out=bf_gate[:], in_=b_f[FEATURES:CHANNELS].partition_broadcast(P))
         load_x(0)
         load_x(1)
         w1_rows = W1_scales.rearrange("g (q r) n -> r q g n", r=4)
@@ -114,9 +116,9 @@ def tile_embed_update_pa_kernel(
             in_=Wf_words.rearrange("g p n t -> p (g n t)").bitcast(I32),
         )
         load_x(4)
-        nc.sync.dma_start(out=bf_bc[:], in_=b_f.partition_broadcast(P))
         for i in range(5, len(LOADS)):
             load_x(i)
+        nc.sync.dma_start(out=bf_bc[:], in_=b_f[0:FEATURES].partition_broadcast(P))
         nc.sync.dma_start(out=emb_sb[:], in_=embeds.rearrange("b s c -> (b s) c"))
         nc.sync.dma_start(out=gamma_bc[:], in_=gamma.partition_broadcast(P))
         nc.sync.dma_start(out=beta_bc[:], in_=beta.partition_broadcast(P))
@@ -274,7 +276,7 @@ def tile_embed_update_pa_kernel(
                     out=sigmoid_of(j),
                     in_=gate.get(j, o_ps[j][:, FEATURES:CHANNELS]),
                     func=ACT.Sigmoid,
-                    bias=bf_bc[:, FEATURES:CHANNELS],
+                    bias=bf_gate[:],
                 )
             for j in links_of(blk):
                 nc.scalar.activation(
@@ -382,28 +384,48 @@ def tile_embed_update_pa_kernel(
                     out=scale[:], in0=totals[:, 1:2], scalar1=inv_l[:], scalar2=inv_l[:], op0=ALU.mult, op1=ALU.mult
                 )
         e_new = consts.tile([P, FEATURES], F32)
-        for cols in halves:
+        e_sums = consts.tile([P, 2], F32)
+        for i, cols in enumerate(halves):
             nc.vector.scalar_tensor_tensor(
-                out=e_new[:, cols], in0=pooled[:, cols], scalar=scale[:], in1=emb_sb[:, cols], op0=ALU.mult, op1=ALU.add
+                out=e_new[:, cols],
+                in0=pooled[:, cols],
+                scalar=scale[:],
+                in1=emb_sb[:, cols],
+                op0=ALU.mult,
+                op1=ALU.add,
+                accum_out=e_sums[:, i : i + 1],
             )
 
         stats = consts.tile([P, 2, 6], F32)
-        for i, cols in enumerate(halves):
-            nc.vector.bn_stats(out=stats[:, i, :], in_=e_new[:, cols])
-        mean_var = consts.tile([P, 2], F32)
-        nc.vector.bn_aggr(out=mean_var[:], in_=stats[:].rearrange("p a b -> p (a b)"))
-        rstd = consts.tile([P, 1], F32)
-        nc.scalar.activation(out=rstd[:], in_=mean_var[:, 1:2], func=ACT.Abs_reciprocal_sqrt, bias=ln_eps[:])
+        mean = consts.tile([P, 1], F32)
+        nc.vector.bn_stats(out=stats[:, 0, :], in_=e_new[:, halves[0]])
+        nc.vector.tensor_scalar(
+            out=mean[:],
+            in0=e_sums[:, 0:1],
+            scalar1=e_sums[:, 1:2],
+            scalar2=1.0 / FEATURES,
+            op0=ALU.add,
+            op1=ALU.mult,
+        )
+        nc.vector.bn_stats(out=stats[:, 1, :], in_=e_new[:, halves[1]])
         centred = consts.tile([P, FEATURES], F32)
-        for cols in halves:
+
+        def centre(cols):
             nc.vector.scalar_tensor_tensor(
                 out=centred[:, cols],
                 in0=e_new[:, cols],
-                scalar=mean_var[:, 0:1],
+                scalar=mean[:],
                 in1=gamma_bc[:, cols],
                 op0=ALU.subtract,
                 op1=ALU.mult,
             )
+
+        centre(halves[0])
+        mean_var = consts.tile([P, 2], F32)
+        nc.vector.bn_aggr(out=mean_var[:], in_=stats[:].rearrange("p a b -> p (a b)"))
+        rstd = consts.tile([P, 1], F32)
+        nc.scalar.activation(out=rstd[:], in_=mean_var[:, 1:2], func=ACT.Abs_reciprocal_sqrt, bias=ln_eps[:])
+        centre(halves[1])
         result = consts.tile([P, FEATURES], F32)
         out_rows = out.rearrange("b s c -> (b s) c")
         for cols, queue in zip(halves, (nc.sync, nc.scalar)):

@@ -33,7 +33,8 @@ HALF = 256
 GATE_COLS = 64
 RUN = 4
 LOADS = (1, 2, 1, 2, 2, 2, 2, 2, 2)
-WARM_UP = 3
+WARM_UP = 4
+WARM_BEHIND = {0: 2, 2: 2}
 M1_LAG = 1
 M2_LAG = 2
 
@@ -65,8 +66,12 @@ def tile_embed_update_pa_kernel(
         zeros = consts.tile([P, CHANNELS], BF16)
         nc.gpsimd.memset(zeros[:], 0.0)
         warm_ps = psum.tile([P, CHANNELS], F32, name="o_ps", bufs=4)
-        for i in range(WARM_UP):
-            nc.tensor.matmul(out=warm_ps[:], lhsT=zeros[:, 0:P], rhs=zeros[:], start=True, stop=True)
+
+        def warm_up(times):
+            for i in range(times):
+                nc.tensor.matmul(out=warm_ps[:], lhsT=zeros[:, 0:P], rhs=zeros[:], start=True, stop=True)
+
+        warm_up(WARM_UP)
         ident = consts.tile([P, P], F32)
         make_identity(nc, ident[:])
         minus_half = consts.tile([P, 1], F32)
@@ -180,6 +185,7 @@ def tile_embed_update_pa_kernel(
                         nc.tensor.transpose(
                             xt_ps[j][:, g, u, :], words[:, first : (g + 1) * (K_PASS // 2) : 2], ident[:]
                         )
+                warm_up(WARM_BEHIND.get(j, 0))
                 nc.scalar.copy(
                     out=x_grouped[blk][:, :, i * P : (i + 1) * P, :].bitcast(F32),
                     in_=xt_ps[j][:].rearrange("p g u r -> p g r u"),

from contextlib import ExitStack

import concourse.mybir as mybir
from concourse.masks import make_identity

F32 = mybir.dt.float32
BF16 = mybir.dt.bfloat16
I32 = mybir.dt.int32
U32 = mybir.dt.uint32
U8 = mybir.dt.uint8
FP8X4 = mybir.dt.float8_e4m3fn_x4
ALU = mybir.AluOpType
ACT = mybir.ActivationFunctionType
AXIS = mybir.AxisListType

P = 128
LINKS = 16
IN = 1024
HID = 512
CHANNELS = 512
FEATURES = CHANNELS - 1
PACK = 4
K_PASS = P * PACK
IN_PASSES = IN // K_PASS
LN_EPS = 1e-5
LINK_EPS = 1e-8

BLOCK_LINKS = 2
BLOCKS = LINKS // BLOCK_LINKS
ROWS = BLOCK_LINKS * P
EARLY = LINKS - BLOCK_LINKS
HALF = 256
GATE_COLS = 64
RUN = 4
LOADS = (1, 2, 1, 2, 2, 2, 2, 2, 2)
WARM_UP = 4
WARM_BEHIND = {0: 2, 2: 2}
M1_LAG = 1
M2_LAG = 2

FLOPS = 2 * P * LINKS * (IN * HID + HID * CHANNELS)


def tile_embed_update_pa_kernel(
    tc, net_in, embeds, m, W1_words, W1_scales, b1, Wf_words, Wf_scales, b_f, gamma, beta, out
):
    nc = tc.nc
    with ExitStack() as stack:
        consts = stack.enter_context(tc.tile_pool(name="consts", bufs=1))
        work = stack.enter_context(tc.tile_pool(name="work", bufs=3))
        psum = stack.enter_context(tc.psum_pool(name="psum", bufs=2))
        stack.enter_context(tc.manual_schedule())

        x_dram = net_in.rearrange("b s l k -> (b s) l k")
        x_sb, x_tiles = [], []
        for n in LOADS:
            x_tiles.append(consts.tile([P, n, IN], BF16, name="x%d" % len(x_sb)))
            x_sb.extend([x_tiles[-1][:, i, :] for i in range(n)])

        def load_x(i):
            first = sum(LOADS[:i])
            nc.sync.dma_start(out=x_tiles[i][:], in_=x_dram[:, first : first + LOADS[i], :])

        planes = consts.tile([P, IN_PASSES + 1, HID], U8, align_bytes=64)
        nc.vector.memset(planes[:].bitcast(I32), 0)
        zeros = consts.tile([P, CHANNELS], BF16)
        nc.gpsimd.memset(zeros[:], 0.0)
        warm_ps = psum.tile([P, CHANNELS], F32, name="o_ps", bufs=4)

        def warm_up(times):
            for i in range(times):
                nc.tensor.matmul(out=warm_ps[:], lhsT=zeros[:, 0:P], rhs=zeros[:], start=True, stop=True)

        warm_up(WARM_UP)
        ident = consts.tile([P, P], F32)
        make_identity(nc, ident[:])
        minus_half = consts.tile([P, 1], F32)
        nc.gpsimd.memset(minus_half[:], -0.5)
        ln_eps = consts.tile([P, 1], F32)
        nc.gpsimd.tensor_scalar(
            out=ln_eps[:], in0=minus_half[:], scalar1=0.0, scalar2=LN_EPS, op0=ALU.mult, op1=ALU.add
        )

        link_eps = consts.tile([P, 1], F32)
        nc.gpsimd.tensor_scalar(
            out=link_eps[:], in0=minus_half[:], scalar1=0.0, scalar2=LINK_EPS, op0=ALU.mult, op1=ALU.add
        )

        w1_raw = consts.tile([P, IN_PASSES, HID], I32)
        wf_words = consts.tile([P, CHANNELS], U32, align_bytes=64)
        m_sb = consts.tile([P, LINKS], BF16)
        b1_sb = consts.tile([P, PACK], BF16)
        bf_bc = consts.tile([P, FEATURES], BF16)
        bf_gate = consts.tile([P, 1], BF16)
        emb_sb = consts.tile([P, FEATURES], BF16)
        gamma_bc = consts.tile([P, FEATURES], BF16)
        beta_bc = consts.tile([P, FEATURES], BF16)

        nc.gpsimd.dma_start(out=b1_sb[:], in_=b1.rearrange("(p t) -> p t", t=PACK))
        nc.gpsimd.dma_start(out=m_sb[:], in_=m.rearrange("b s l o -> (b s) (l o)"))
        nc.gpsimd.dma_start(out=bf_gate[:], in_=b_f[FEATURES:CHANNELS].partition_broadcast(P))
        load_x(0)
        load_x(1)
        w1_rows = W1_scales.rearrange("g (q r) n -> r q g n", r=4)
        for r in range(4):
            nc.sync.dma_start(
                out=planes[r:P:32, 0:IN_PASSES, :].bitcast(I32), in_=w1_rows[r].bitcast(I32)
            )
        nc.sync.dma_start(
            out=w1_raw[:], in_=W1_words.rearrange("g p n t -> p g (n t)").bitcast(I32)
        )
        load_x(2)
        load_x(3)
        wf_rows = Wf_scales.rearrange("g (q r) n -> r q (g n)", r=4)
        for r in range(4):
            nc.sync.dma_start(
                out=planes[r:P:32, IN_PASSES, :].bitcast(I32), in_=wf_rows[r].bitcast(I32)
            )
        nc.sync.dma_start(
            out=wf_words[:].bitcast(I32),
            in_=Wf_words.rearrange("g p n t -> p (g n t)").bitcast(I32),
        )
        load_x(4)
        for i in range(5, len(LOADS)):
            load_x(i)
        nc.sync.dma_start(out=bf_bc[:], in_=b_f[0:FEATURES].partition_broadcast(P))
        nc.sync.dma_start(out=emb_sb[:], in_=embeds.rearrange("b s c -> (b s) c"))
        nc.sync.dma_start(out=gamma_bc[:], in_=gamma.partition_broadcast(P))
        nc.sync.dma_start(out=beta_bc[:], in_=beta.partition_broadcast(P))

        table_warm = consts.tile([P, 1], F32)
        nc.scalar.activation(out=table_warm[:], in_=minus_half[:], func=ACT.Sigmoid)

        m_sq = consts.tile([P, LINKS], F32)
        nc.gpsimd.tensor_tensor(out=m_sq[:], in0=m_sb[:], in1=m_sb[:], op=ALU.mult)
        m_eps = consts.tile([P, LINKS], F32)
        nc.gpsimd.tensor_scalar(
            out=m_eps[:], in0=m_sb[:], scalar1=LINK_EPS, scalar2=0.0, op0=ALU.mult, op1=ALU.add
        )
        m_late = consts.tile([P, BLOCK_LINKS], F32)
        nc.gpsimd.tensor_scalar(
            out=m_late[:], in0=m_sb[:, EARLY:LINKS], scalar1=1.0, scalar2=0.0, op0=ALU.mult, op1=ALU.add
        )

        w1_cols = consts.tile([P, IN_PASSES, PACK, P], I32, align_bytes=64)
        w1_planes = consts.tile([P, IN_PASSES, PACK, P], U8, align_bytes=64)
        raw_planes = planes[:, 0:IN_PASSES, :].rearrange("p g (m t) -> p g m t", t=PACK)
        raw_words = w1_raw[:].rearrange("p g (m t) -> p g m t", t=PACK)
        for t in range(PACK):
            nc.vector.tensor_copy(out=w1_planes[:, :, t, :], in_=raw_planes[:, :, :, t])

        def sort_words(slots):
            for t in slots:
                nc.vector.tensor_copy(out=w1_cols[:, :, t, :], in_=raw_words[:, :, :, t])


        sig = consts.tile([P, LINKS], F32)
        terms = consts.tile([P, 3, LINKS], F32)
        acc = consts.tile([P, FEATURES], F32)
        nc.gpsimd.memset(sig[:, EARLY:LINKS], 0.0)
        nc.gpsimd.tensor_scalar(
            out=terms[:, 2, EARLY:LINKS], in0=m_eps[:, EARLY:LINKS], scalar1=1.0, scalar2=0.0, op0=ALU.mult, op1=ALU.add
        )
        g_all = consts.tile([P, LINKS], F32)
        sums = consts.tile([P, 1 + BLOCK_LINKS, 3], F32)
        late = consts.tile([P, 4, BLOCK_LINKS], F32)
        xt_ps, x_grouped, x_codes, x_scales = {}, {}, {}, {}
        h_ps, h_slots, h_grouped, h_codes, h_scales, o_ps = {}, {}, {}, {}, {}, {}

        def links_of(blk):
            if 0 <= blk < BLOCKS:
                return range(blk * BLOCK_LINKS, (blk + 1) * BLOCK_LINKS)
            return range(0)

        def transpose_x(blk):
            if len(links_of(blk)) == 0:
                return
            x_grouped[blk] = work.tile([P, IN_PASSES, ROWS, PACK], BF16, name="x_grouped", align_bytes=64)
            for i, j in enumerate(links_of(blk)):
                words = x_sb[j].bitcast(F32)
                xt_ps[j] = psum.tile([P, IN_PASSES, 2, P], F32, name="xt_ps")
                for g in range(IN_PASSES):
                    for u in range(2):
                        first = g * (K_PASS // 2) + u
                        nc.tensor.transpose(
                            xt_ps[j][:, g, u, :], words[:, first : (g + 1) * (K_PASS // 2) : 2], ident[:]
                        )
                warm_up(WARM_BEHIND.get(j, 0))
                nc.scalar.copy(
                    out=x_grouped[blk][:, :, i * P : (i + 1) * P, :].bitcast(F32),
                    in_=xt_ps[j][:].rearrange("p g u r -> p g r u"),
                )

        def quantise_x(blk):
            if len(links_of(blk)) == 0:
                return
            x_codes[blk] = work.tile([P, IN_PASSES, ROWS], U32, name="x_codes", align_bytes=64)
            x_scales[blk] = work.tile([P, IN_PASSES, ROWS], U8, name="x_scales", align_bytes=64)
            nc.vector.quantize_mx(
                out=x_codes[blk][:].rearrange("p g r -> p (g r)").bitcast(FP8X4),
                scales=x_scales[blk][:].rearrange("p g r -> p (g r)"),
                in_=x_grouped[blk][:].rearrange("p g r t -> p (g r t)"),
            )

        def first_matmul(blk):
            if len(links_of(blk)) == 0:
                return
            h_slots[blk] = work.tile([P, PACK, ROWS], BF16, name="h_slots")
            for half in range(PACK // 2):
                h_ps[blk, half] = psum.tile([P, 2, ROWS], F32, name="h_ps")
                for s in range(2):
                    t = 2 * half + s
                    for g in range(IN_PASSES):
                        nc.tensor.matmul_mx(
                            out=h_ps[blk, half][:, s, :],
                            lhsT=w1_cols[:, g, t, :].bitcast(FP8X4),
                            lhsT_scale=w1_planes[:, g, t, :],
                            rhs=x_codes[blk][:, g, :].bitcast(FP8X4),
                            rhs_scale=x_scales[blk][:, g, :],
                            start=(g == 0),
                            stop=(g == IN_PASSES - 1),
                        )
                for s in range(2):
                    t = 2 * half + s
                    nc.scalar.activation(
                        out=h_slots[blk][:, t, :],
                        in_=h_ps[blk, half][:, s, :],
                        func=ACT.Relu,
                        bias=b1_sb[:, t : t + 1],
                    )

        def group_h(blk):
            if len(links_of(blk)) == 0:
                return
            h_grouped[blk] = work.tile([P, ROWS, PACK], BF16, name="h_grouped", align_bytes=64)
            nc.vector.tensor_copy(
                out=h_grouped[blk][:].rearrange("p (c i) t -> p c t i", i=RUN),
                in_=h_slots[blk][:].rearrange("p t (c i) -> p c t i", i=RUN),
            )

        def quantise_h(blk):
            if len(links_of(blk)) == 0:
                return
            h_codes[blk] = work.tile([P, ROWS], U32, name="h_codes", align_bytes=64)
            h_scales[blk] = work.tile([P, ROWS], U8, name="h_scales", align_bytes=64)
            nc.vector.quantize_mx(
                out=h_codes[blk][:].bitcast(FP8X4),
                scales=h_scales[blk][:],
                in_=h_grouped[blk][:].rearrange("p r t -> p (r t)"),
            )

        def sigmoid_of(j):
            return sig[:, j : j + 1] if j < EARLY else late[:, 0, j - EARLY : j - EARLY + 1]

        def weight_of(j):
            return terms[:, 2, j : j + 1] if j < EARLY else late[:, 1, j - EARLY : j - EARLY + 1]

        def second_pass(blk, i, out, cols):
            tokens = slice(i * P, (i + 1) * P)
            nc.tensor.matmul_mx(
                out=out,
                lhsT=h_codes[blk][:, tokens].bitcast(FP8X4),
                lhsT_scale=h_scales[blk][:, tokens],
                rhs=wf_words[:, cols].bitcast(FP8X4),
                rhs_scale=planes[:, IN_PASSES, cols],
                start=True,
                stop=True,
            )

        def second_matmul(blk):
            gate = {}
            if blk == BLOCKS - 1:
                for i, j in enumerate(links_of(blk)):
                    gate_ps = psum.tile([P, GATE_COLS], F32, name="xt_ps")
                    second_pass(blk, i, gate_ps[:], slice(CHANNELS - GATE_COLS, CHANNELS))
                    gate[j] = gate_ps[:, GATE_COLS - 1 : GATE_COLS]
            for i, j in enumerate(links_of(blk)):
                o_ps[j] = psum.tile([P, CHANNELS], F32, name="o_ps", bufs=4)
                second_pass(blk, i, o_ps[j][:], slice(0, CHANNELS))
            for j in links_of(blk):
                nc.scalar.activation(
                    out=sigmoid_of(j),
                    in_=gate.get(j, o_ps[j][:, FEATURES:CHANNELS]),
                    func=ACT.Sigmoid,
                    bias=bf_gate[:],
                )
            for j in links_of(blk):
                nc.scalar.activation(
                    out=weight_of(j),
                    in_=sigmoid_of(j),
                    func=ACT.Identity,
                    scale=m_sq[:, j : j + 1],
                    bias=m_eps[:, j : j + 1],
                )

        def pool_columns(j, cols):
            if j == 0:
                nc.vector.tensor_scalar_mul(out=acc[:, cols], in0=o_ps[j][:, cols], scalar1=weight_of(j))
            else:
                nc.vector.scalar_tensor_tensor(
                    out=acc[:, cols],
                    in0=o_ps[j][:, cols],
                    scalar=weight_of(j),
                    in1=acc[:, cols],
                    op0=ALU.mult,
                    op1=ALU.add,
                )

        def pool_link(blk, i):
            if 0 <= blk:
                pool_columns(links_of(blk)[i], slice(0, FEATURES))

        sort_words(range(1))
        transpose_x(0)
        quantise_x(0)
        sort_words(range(1, PACK))
        for step in range(1, BLOCKS):
            if step < BLOCKS - 1:
                transpose_x(step)
            first_matmul(step - M1_LAG)
            second_matmul(step - M2_LAG)
            if step < BLOCKS - 1:
                quantise_x(step)
            group_h(step - M1_LAG)
            pool_link(step - M2_LAG, 0)
            quantise_h(step - M1_LAG)
            if step == BLOCKS - 2:
                transpose_x(step + 1)
                quantise_x(step + 1)
            pool_link(step - M2_LAG, 1)

        halves = (slice(0, HALF), slice(HALF, FEATURES))
        last = BLOCKS - 1
        before = links_of(last - 1)
        first_matmul(last)
        second_matmul(last - 1)
        group_h(last)
        pool_columns(before[0], halves[0])
        quantise_h(last)
        second_matmul(last)
        nc.vector.tensor_tensor(out=g_all[:], in0=sig[:], in1=m_sb[:], op=ALU.mult)
        pool_columns(before[0], halves[1])
        nc.vector.tensor_scalar_add(out=terms[:, 0, :], in0=g_all[:], scalar1=LINK_EPS)
        pool_columns(before[1], halves[0])
        nc.vector.tensor_tensor(out=terms[:, 1, :], in0=terms[:, 0, :], in1=g_all[:], op=ALU.mult)
        pool_columns(before[1], halves[1])
        nc.vector.tensor_reduce(out=sums[:, 0, :], in_=terms[:], axis=AXIS.X, op=ALU.add)
        for i in range(BLOCK_LINKS):
            nc.scalar.activation(
                out=late[:, 2, i : i + 1], in_=sigmoid_of(EARLY + i), func=ACT.Copy, scale=m_late[:, i : i + 1]
            )
            nc.scalar.activation(
                out=late[:, 3, i : i + 1],
                in_=sigmoid_of(EARLY + i),
                func=ACT.Identity,
                scale=m_late[:, i : i + 1],
                bias=link_eps[:],
            )
        for i in range(BLOCK_LINKS):
            for s, (factor, part) in enumerate(
                (
                    (m_late[:, i : i + 1], sigmoid_of(EARLY + i)),
                    (late[:, 2, i : i + 1], late[:, 3, i : i + 1]),
                    (m_sq[:, EARLY + i : EARLY + i + 1], sigmoid_of(EARLY + i)),
                )
            ):
                nc.scalar.activation(
                    out=sums[:, i + 1, s : s + 1],
                    in_=part,
                    func=ACT.Identity,
                    scale=factor,
                    bias=sums[:, i, s : s + 1],
                )
        totals = sums[:, BLOCK_LINKS, :]
        nc.scalar.activation(out=table_warm[:], in_=ln_eps[:], func=ACT.Abs_reciprocal_sqrt)
        inv_l = consts.tile([P, 1], F32)
        pool_columns(EARLY, halves[0])
        pool_columns(EARLY, halves[1])
        pool_columns(EARLY + 1, halves[0])
        nc.vector.reciprocal(out=inv_l[:], in_=totals[:, 0:1])
        pool_columns(EARLY + 1, halves[1])
        pooled = consts.tile([P, FEATURES], F32)
        scale = consts.tile([P, 1], F32)
        for cols in halves:
            nc.vector.scalar_tensor_tensor(
                out=pooled[:, cols], in0=bf_bc[:, cols], scalar=totals[:, 2:3], in1=acc[:, cols], op0=ALU.mult, op1=ALU.add
            )
            if cols == halves[0]:
                nc.vector.tensor_scalar(
                    out=scale[:], in0=totals[:, 1:2], scalar1=inv_l[:], scalar2=inv_l[:], op0=ALU.mult, op1=ALU.mult
                )
        e_new = consts.tile([P, FEATURES], F32)
        e_sums = consts.tile([P, 2], F32)
        for i, cols in enumerate(halves):
            nc.vector.scalar_tensor_tensor(
                out=e_new[:, cols],
                in0=pooled[:, cols],
                scalar=scale[:],
                in1=emb_sb[:, cols],
                op0=ALU.mult,
                op1=ALU.add,
                accum_out=e_sums[:, i : i + 1],
            )

        stats = consts.tile([P, 2, 6], F32)
        mean = consts.tile([P, 1], F32)
        nc.vector.bn_stats(out=stats[:, 0, :], in_=e_new[:, halves[0]])
        nc.vector.tensor_scalar(
            out=mean[:],
            in0=e_sums[:, 0:1],
            scalar1=e_sums[:, 1:2],
            scalar2=1.0 / FEATURES,
            op0=ALU.add,
            op1=ALU.mult,
        )
        nc.vector.bn_stats(out=stats[:, 1, :], in_=e_new[:, halves[1]])
        centred = consts.tile([P, FEATURES], F32)

        def centre(cols):
            nc.vector.scalar_tensor_tensor(
                out=centred[:, cols],
                in0=e_new[:, cols],
                scalar=mean[:],
                in1=gamma_bc[:, cols],
                op0=ALU.subtract,
                op1=ALU.mult,
            )

        centre(halves[0])
        mean_var = consts.tile([P, 2], F32)
        nc.vector.bn_aggr(out=mean_var[:], in_=stats[:].rearrange("p a b -> p (a b)"))
        rstd = consts.tile([P, 1], F32)
        nc.scalar.activation(out=rstd[:], in_=mean_var[:, 1:2], func=ACT.Abs_reciprocal_sqrt, bias=ln_eps[:])
        centre(halves[1])
        result = consts.tile([P, FEATURES], F32)
        out_rows = out.rearrange("b s c -> (b s) c")
        for cols, queue in zip(halves, (nc.sync, nc.scalar)):
            nc.vector.scalar_tensor_tensor(
                out=result[:, cols], in0=centred[:, cols], scalar=rstd[:], in1=beta_bc[:, cols], op0=ALU.mult, op1=ALU.add
            )
            queue.dma_start(out=out_rows[:, cols], in_=result[:, cols])
